import numpy as np
import ml_dtypes


def mxq(x, axis, fmt="e4m3"):
    dtype, down = {"e4m3": (ml_dtypes.float8_e4m3fn, 7), "e5m2": (ml_dtypes.float8_e5m2, 14)}[fmt]
    v = np.moveaxis(np.asarray(x, np.float32).astype(ml_dtypes.bfloat16).astype(np.float64), axis, -1)
    blocks = v.reshape(v.shape[:-1] + (-1, 32))
    amax = np.abs(blocks).max(-1, keepdims=True)
    byte = np.maximum(np.where(amax > 0, np.frexp(amax)[1] - 1 + 127, 0) - down, 1)
    scale = np.exp2(byte - 127.0)
    codes = (blocks / scale).astype(np.float32).astype(dtype).astype(np.float64)
    return np.moveaxis((codes * scale).reshape(v.shape), -1, axis)


WIDE = False


def mx_kscale(k):
    if not WIDE:
        return np.ones(k)
    levels = np.array([10, -10, 5, -5, 0])
    a = np.random.permutation(np.resize(levels, k // 512 * 4)).reshape(k // 512, 4)
    idx = np.arange(k)
    return np.exp2(a[idx // 512, idx % 128 // 32])


BF16 = ml_dtypes.bfloat16


def bf(x):
    return np.asarray(x, np.float32).astype(BF16)


def f64(x):
    return np.asarray(x).astype(np.float64)


B, S, IN, OUT, SPLIT = 2, 512, 2048, 2048, 512


def binarise(w):
    return np.sign(w)


def branch(x2d, V, U, v2, v1, u2, u1):
    v1u2 = v1 * u2
    h = mxq(x2d * v2, 1, "e4m3") @ mxq(binarise(V), 1, "e4m3").T
    return (mxq(h * v1u2, 1, "e4m3") @ mxq(binarise(U), 1, "e4m3").T) * u1


def setup_inputs():
    n = np.random.standard_normal
    s, t = mx_kscale(IN), mx_kscale(SPLIT)
    rs = s[np.arange(SPLIT) * IN // SPLIT]
    rt = t[np.arange(OUT) * SPLIT // OUT]
    mv = np.where(rs[:, None] == s[None, :], 1.0, 0.0)
    mu = np.where(rt[:, None] == t[None, :], 1.0, 0.0)
    gv = np.sqrt(IN / mv.sum(1))
    gu = np.sqrt(SPLIT / mu.sum(1))
    return {
        "x": bf(n((B, S, IN))),
        "V": bf(n((SPLIT, IN)) * mv),
        "U": bf(n((OUT, SPLIT)) * mu),
        "v2": bf(n((1, IN)) * 5.0 / np.sqrt(IN) * s),
        "v1": bf(n((1, SPLIT)) * 0.3 * gv / rs),
        "u2": bf(n((1, SPLIT)) * 0.3 * t),
        "u1": bf(n((1, OUT)) * 3.0 / np.sqrt(SPLIT) * gu / rt),
        "V_R": bf(n((SPLIT, IN)) * mv),
        "U_R": bf(n((OUT, SPLIT)) * mu),
        "v2_R": bf(n((1, IN)) * 5.0 / np.sqrt(IN) * s),
        "v1_R": bf(n((1, SPLIT)) * 0.3 * gv / rs),
        "u2_R": bf(n((1, SPLIT)) * 0.3 * t),
        "u1_R": bf(n((1, OUT)) * 3.0 / np.sqrt(SPLIT) * gu / rt),
        "bias": bf(n(OUT) * 0.3),
    }


def reference(x, V, U, v2, v1, u2, u1, V_R, U_R, v2_R, v1_R, u2_R, u1_R, bias):
    x = f64(x)
    lead = x.shape[:-1]
    x2d = x.reshape(-1, x.shape[-1])
    y = branch(x2d, f64(V), f64(U), f64(v2), f64(v1), f64(u2), f64(u1))
    y = y + branch(x2d, f64(V_R), f64(U_R), f64(v2_R), f64(v1_R), f64(u2_R), f64(u1_R))
    y = y + f64(bias)
    return y.reshape(lead + (U.shape[0],))

@@ -1,0 +1,282 @@
+from contextlib import ExitStack
+
+import concourse.mybir as mybir
+from concourse.masks import make_identity
+
+F32 = mybir.dt.float32
+BF16 = mybir.dt.bfloat16
+U32 = mybir.dt.uint32
+U8 = mybir.dt.uint8
+FP8X4 = mybir.dt.float8_e4m3fn_x4
+ACT = mybir.ActivationFunctionType
+ALU = mybir.AluOpType
+
+P = 128
+PACK = 4
+K_PASS = P * PACK
+BANK = 512
+
+ROWS, IN, SPLIT, OUT = 1024, 2048, 512, 2048
+BRANCHES = 2
+PASSES = IN // K_PASS
+UNITS = 4
+HALVES = ROWS // BANK
+X_TILES = BANK // P
+S_TILES = SPLIT // P
+O_GROUPS = OUT // BANK
+O_TILES = BANK // P
+RAW_SLOTS = 14
+WEIGHTS_PER_X_TILE = 3
+
+FLOPS = 2 * BRANCHES * (ROWS * IN * SPLIT + ROWS * SPLIT * OUT)
+
+
+def tile_littlebititqspeclinear_pa_kernel(
+    tc, x, V, U, v2, v1, u2, u1, V_R, U_R, v2_R, v1_R, u2_R, u1_R, bias, out
+):
+    nc = tc.nc
+    x_rows = x.flatten_outer_dims()
+    out_rows = out.flatten_outer_dims()
+
+    with ExitStack() as ctx:
+        consts = ctx.enter_context(tc.tile_pool(name="consts", bufs=1))
+        keep = ctx.enter_context(tc.tile_pool(name="keep", bufs=1))
+        raws = ctx.enter_context(tc.tile_pool(name="raws", bufs=RAW_SLOTS))
+        stage = ctx.enter_context(tc.tile_pool(name="stage", bufs=2))
+        psum_w = ctx.enter_context(tc.psum_pool(name="psum_w", bufs=2))
+        psum_x = ctx.enter_context(tc.psum_pool(name="psum_x", bufs=2))
+        psum_acc = ctx.enter_context(tc.psum_pool(name="psum_acc", bufs=4))
+
+        ident_f32 = consts.tile([P, P], F32)
+        make_identity(nc, ident_f32[:])
+        ident_bf16 = consts.tile([P, P], BF16)
+        make_identity(nc, ident_bf16[:])
+
+        word_rows = consts.tile([P, 2 * P], BF16)
+        nc.vector.memset(word_rows[:], 0.0)
+        first_row = 0
+        for vector in (v2, v2_R, v1, u2, v1_R, u2_R):
+            rows = vector.rearrange("o (c w) -> (o c) w", w=2 * P)
+            nc.sync.dma_start(out=word_rows[first_row : first_row + rows.shape[0], :], in_=rows)
+            first_row += rows.shape[0]
+        WORD_COLS = 2 * first_row
+
+        out_vec_rows = consts.tile([P, P], BF16)
+        nc.vector.memset(out_vec_rows[:], 0.0)
+        OUT_COLS = OUT // P
+        nc.gpsimd.dma_start(out=out_vec_rows[0:OUT_COLS, :], in_=u1.rearrange("o (c w) -> (o c) w", w=P))
+        nc.gpsimd.dma_start(
+            out=out_vec_rows[OUT_COLS : 2 * OUT_COLS, :], in_=u1_R.rearrange("o (c w) -> (o c) w", w=P)
+        )
+        nc.gpsimd.dma_start(
+            out=out_vec_rows[2 * OUT_COLS : 3 * OUT_COLS, :], in_=bias.rearrange("(c w) -> c w", w=P)
+        )
+
+        weight_views = []
+        for matrix in (V, V_R):
+            by_code = matrix.rearrange("(u p e) k -> u e p k", u=2, e=2)
+            for t in range(S_TILES):
+                weight_views.append(by_code[t // 2, t % 2])
+        for og in range(O_GROUPS):
+            for matrix in (U, U_R):
+                weight_views.append(matrix.rearrange("(g n p) s -> g p n s", n=O_TILES, p=P)[og])
+        x_views = x_rows.rearrange("(n p) k -> n p k", p=P)
+
+        def load_weight(w):
+            raw = raws.tile([P, IN], BF16, tag="raw", name="raw_w%d" % w)
+            if w < BRANCHES * S_TILES:
+                nc.sync.dma_start(out=raw[:], in_=weight_views[w])
+            else:
+                nc.sync.dma_start(out=raw[:].rearrange("p (n s) -> p n s", n=O_TILES), in_=weight_views[w])
+            return raw
+
+        def load_x(rt):
+            raw = raws.tile([P, IN], BF16, tag="raw", name="raw_x%d" % rt)
+            nc.sync.dma_start(out=raw[:], in_=x_views[rt])
+            return raw
+
+        raw_w = {}
+        raw_x = {}
+        EARLY_WEIGHTS = WEIGHTS_PER_X_TILE * X_TILES
+        for j in range(X_TILES):
+            raw_w[WEIGHTS_PER_X_TILE * j] = load_weight(WEIGHTS_PER_X_TILE * j)
+            raw_x[j] = load_x(j)
+            for w in range(WEIGHTS_PER_X_TILE * j + 1, WEIGHTS_PER_X_TILE * (j + 1)):
+                raw_w[w] = load_weight(w)
+        for j in range(X_TILES):
+            raw_w[EARLY_WEIGHTS + j] = load_weight(EARLY_WEIGHTS + j)
+            raw_x[X_TILES + j] = load_x(X_TILES + j)
+
+        word_bank = psum_x.tile([P, BANK], F32, tag="tx")
+        nc.tensor.transpose(word_bank[:, 0:P], word_rows[:].bitcast(F32), ident_f32[:])
+        k_vectors = consts.tile([P, WORD_COLS], BF16)
+        nc.vector.tensor_copy(out=k_vectors[:], in_=word_bank[:].bitcast(BF16)[:, 0:WORD_COLS])
+        V2_COLS = BRANCHES * PASSES * PACK
+        v1_and_u2 = k_vectors[:, V2_COLS:WORD_COLS].rearrange("p (b w t) -> p b w t", b=BRANCHES, w=2)
+        v1u2 = consts.tile([P, BRANCHES, PACK], F32)
+        nc.vector.tensor_tensor(out=v1u2[:], in0=v1_and_u2[:, :, 0, :], in1=v1_and_u2[:, :, 1, :], op=ALU.mult)
+
+        out_vec_bank = psum_x.tile([P, P], BF16, tag="tx")
+        nc.tensor.transpose(out_vec_bank[:], out_vec_rows[:], ident_bf16[:])
+        o_vectors = consts.tile([P, 3, OUT_COLS], F32)
+        nc.vector.tensor_copy(
+            out=o_vectors[:].rearrange("p v c -> p (v c)"), in_=out_vec_bank[:, 0 : 3 * OUT_COLS]
+        )
+
+        v_codes = [keep.tile([P, S_TILES, K_PASS], U32, name="v_codes%d" % b, align_bytes=64) for b in range(2)]
+        v_scales = [keep.tile([P, S_TILES, K_PASS], U8, name="v_scales%d" % b, align_bytes=64) for b in range(2)]
+        u_codes = [keep.tile([P, O_GROUPS, BANK], U32, name="u_codes%d" % b, align_bytes=64) for b in range(2)]
+        u_scales = [keep.tile([P, O_GROUPS, BANK], U8, name="u_scales%d" % b, align_bytes=64) for b in range(2)]
+        x_codes = {}
+        x_scales = {}
+        h_codes = {}
+        h_scales = {}
+        for b in range(BRANCHES):
+            for h in range(HALVES):
+                x_codes[b, h] = keep.tile([P, PASSES, BANK], U32, name="x_codes%d%d" % (b, h), align_bytes=64)
+                x_scales[b, h] = keep.tile([P, PASSES, BANK], U8, name="x_scales%d%d" % (b, h), align_bytes=64)
+                h_codes[b, h] = keep.tile([P, BANK], U32, name="h_codes%d%d" % (b, h), align_bytes=64)
+                h_scales[b, h] = keep.tile([P, BANK], U8, name="h_scales%d%d" % (b, h), align_bytes=64)
+
+        def transpose_words(raw, pool, tag):
+            words = raw[:].bitcast(F32)
+            banks = []
+            for i in range(2):
+                bank = pool.tile([P, BANK], F32, tag=tag)
+                for j in range(BANK // P):
+                    c = (BANK // P) * i + j
+                    nc.tensor.transpose(bank[:, j * P : (j + 1) * P], words[:, c * P : (c + 1) * P], ident_f32[:])
+                banks.append(bank)
+            return banks
+
+        def unit_by_row(banks, n):
+            half = banks[n // 2][:].bitcast(BF16)[:, (n % 2) * K_PASS : (n % 2 + 1) * K_PASS]
+            return half.rearrange("p (u r e) -> p r u e", u=2, e=2)
+
+        def prepare_weight(w):
+            banks = transpose_words(raw_w[w], psum_w, "tw")
+            signs = stage.tile([P, UNITS, P, PACK], BF16, tag="signs", align_bytes=64)
+            for n in range(UNITS):
+                nc.scalar.activation(
+                    out=signs[:, n, :, :].rearrange("p r (u e) -> p r u e", u=2),
+                    in_=unit_by_row(banks, n),
+                    func=ACT.Sign,
+                )
+            if w < BRANCHES * S_TILES:
+                b, t = w // S_TILES, w % S_TILES
+                codes, scales = v_codes[b][:, t, :], v_scales[b][:, t, :]
+            else:
+                og, b = (w - BRANCHES * S_TILES) // BRANCHES, w % BRANCHES
+                codes, scales = u_codes[b][:, og, :], u_scales[b][:, og, :]
+            nc.vector.quantize_mx(
+                out=codes.bitcast(FP8X4), scales=scales, in_=signs[:].rearrange("p n r t -> p (n r t)")
+            )
+
+        def prepare_x(rt):
+            h, j = rt // X_TILES, rt % X_TILES
+            banks = transpose_words(raw_x[rt], psum_x, "tx")
+            scaled = stage.tile([P, PASSES, BRANCHES, P, PACK], BF16, tag="scaled", align_bytes=64)
+            for g in range(PASSES):
+                for b in range(BRANCHES):
+                    first = (b * PASSES + g) * PACK
+                    factors = k_vectors[:, first : first + PACK].rearrange("p (u e) -> p u e", u=2)
+                    nc.vector.tensor_tensor(
+                        out=scaled[:, g, b, :, :].rearrange("p r (u e) -> p r u e", u=2),
+                        in0=unit_by_row(banks, g),
+                        in1=factors.unsqueeze(1).to_broadcast([P, P, 2, 2]),
+                        op=ALU.mult,
+                    )
+            for g in range(PASSES):
+                for b in range(BRANCHES):
+                    nc.vector.quantize_mx(
+                        out=x_codes[b, h][:, g, j * P : (j + 1) * P].bitcast(FP8X4),
+                        scales=x_scales[b, h][:, g, j * P : (j + 1) * P],
+                        in_=scaled[:, g, b, :, :].rearrange("p r t -> p (r t)"),
+                    )
+
+        def first_stage(h):
+            for b in range(BRANCHES):
+                planes = stage.tile([P, S_TILES, BANK], BF16, tag="planes")
+                for t in range(S_TILES):
+                    acc = psum_acc.tile([P, BANK], F32, tag="acc")
+                    for g in range(PASSES):
+                        nc.tensor.matmul_mx(
+                            out=acc[:],
+                            lhsT=v_codes[b][:, t, g * P : (g + 1) * P].bitcast(FP8X4),
+                            lhsT_scale=v_scales[b][:, t, g * P : (g + 1) * P],
+                            rhs=x_codes[b, h][:, g, :].bitcast(FP8X4),
+                            rhs_scale=x_scales[b, h][:, g, :],
+                            start=(g == 0),
+                            stop=(g == PASSES - 1),
+                        )
+                    nc.scalar.activation(out=planes[:, t, :], in_=acc[:], func=ACT.Copy, scale=v1u2[:, b, t : t + 1])
+                grouped = stage.tile([P, BANK, PACK], BF16, tag="grouped", align_bytes=64)
+                nc.vector.tensor_copy(
+                    out=grouped[:].rearrange("p (c i) t -> p c t i", i=4),
+                    in_=planes[:].rearrange("p t (c i) -> p c t i", i=4),
+                )
+                nc.vector.quantize_mx(
+                    out=h_codes[b, h][:].bitcast(FP8X4),
+                    scales=h_scales[b, h][:],
+                    in_=grouped[:].rearrange("p r t -> p (r t)"),
+                )
+
+        def second_stage(h, og):
+            total = stage.tile([P, O_TILES, BANK], F32, tag="total")
+            for ol in range(O_TILES):
+                ot = og * O_TILES + ol
+                products = []
+                for b in range(BRANCHES):
+                    acc = psum_acc.tile([P, BANK], F32, tag="acc")
+                    nc.tensor.matmul_mx(
+                        out=acc[:],
+                        lhsT=u_codes[b][:, og, ol * P : (ol + 1) * P].bitcast(FP8X4),
+                        lhsT_scale=u_scales[b][:, og, ol * P : (ol + 1) * P],
+                        rhs=h_codes[b, h][:].bitcast(FP8X4),
+                        rhs_scale=h_scales[b, h][:],
+                        start=True,
+                        stop=True,
+                    )
+                    products.append(acc)
+                main = stage.tile([P, BANK], F32, tag="main")
+                nc.scalar.activation(
+                    out=main[:],
+                    in_=products[0][:],
+                    func=ACT.Identity,
+                    scale=o_vectors[:, 0, ot : ot + 1],
+                    bias=o_vectors[:, 2, ot : ot + 1],
+                )
+                nc.vector.scalar_tensor_tensor(
+                    out=total[:, ol, :],
+                    in0=products[1][:],
+                    scalar=o_vectors[:, 1, ot : ot + 1],
+                    in1=main[:],
+                    op0=ALU.mult,
+                    op1=ALU.add,
+                )
+            for j in range(X_TILES):
+                bank = psum_w.tile([P, BANK], F32, tag="tw")
+                for ol in range(O_TILES):
+                    nc.tensor.transpose(
+                        bank[:, ol * P : (ol + 1) * P], total[:, ol, j * P : (j + 1) * P], ident_f32[:]
+                    )
+                result = stage.tile([P, BANK], F32, tag="result", bufs=4)
+                if h == HALVES - 1 and j % 2 == 1:
+                    nc.vector.tensor_copy(out=result[:], in_=bank[:])
+                else:
+                    nc.scalar.copy(out=result[:], in_=bank[:])
+                r0 = h * BANK + j * P
+                nc.sync.dma_start(out=out_rows[r0 : r0 + P, og * BANK : (og + 1) * BANK], in_=result[:])
+
+        for j in range(X_TILES):
+            prepare_x(j)
+            for w in range(WEIGHTS_PER_X_TILE * j, WEIGHTS_PER_X_TILE * (j + 1)):
+                prepare_weight(w)
+        first_stage(0)
+        for j in range(X_TILES):
+            prepare_weight(EARLY_WEIGHTS + j)
+            prepare_x(X_TILES + j)
+            second_stage(0, j)
+        first_stage(1)
+        for og in range(O_GROUPS):
+            second_stage(1, og)

@@ -175,23 +175,28 @@ def tile_littlebititqspeclinear_pa_kernel(
         def prepare_x(rt):
             h, j = rt // X_TILES, rt % X_TILES
             banks = transpose_words(raw_x[rt], psum_x, "tx")
-            scaled = stage.tile([P, PASSES, BRANCHES, P, PACK], BF16, tag="scaled", align_bytes=64)
-            for g in range(PASSES):
-                for b in range(BRANCHES):
-                    first = (b * PASSES + g) * PACK
-                    factors = k_vectors[:, first : first + PACK].rearrange("p (u e) -> p u e", u=2)
-                    nc.vector.tensor_tensor(
-                        out=scaled[:, g, b, :, :].rearrange("p r (u e) -> p r u e", u=2),
-                        in0=unit_by_row(banks, g),
-                        in1=factors.unsqueeze(1).to_broadcast([P, P, 2, 2]),
-                        op=ALU.mult,
-                    )
-            for g in range(PASSES):
-                for b in range(BRANCHES):
+            grouped = stage.tile([P, IN // 2], F32, tag="x_grouped")
+            by_pass = grouped[:].rearrange("p (g r u) -> p g r u", g=PASSES, u=2)
+            for i in range(2):
+                nc.vector.tensor_copy(
+                    out=by_pass[:, 2 * i : 2 * i + 2, :, :],
+                    in_=banks[i][:].rearrange("p (g u r) -> p g r u", g=2, u=2),
+                )
+            scaled = stage.tile([P, BRANCHES, PASSES, P, PACK], BF16, tag="scaled", align_bytes=64)
+            for b in range(BRANCHES):
+                factors = k_vectors[:, b * PASSES * PACK : (b + 1) * PASSES * PACK]
+                nc.vector.tensor_tensor(
+                    out=scaled[:, b, :, :, :],
+                    in0=grouped[:].bitcast(BF16).rearrange("p (g r t) -> p g r t", g=PASSES, t=PACK),
+                    in1=factors.rearrange("p (g t) -> p g t", g=PASSES).unsqueeze(2).to_broadcast([P, PASSES, P, PACK]),
+                    op=ALU.mult,
+                )
+            for b in range(BRANCHES):
+                for g in range(PASSES):
                     nc.vector.quantize_mx(
                         out=x_codes[b, h][:, g, j * P : (j + 1) * P].bitcast(FP8X4),
                         scales=x_scales[b, h][:, g, j * P : (j + 1) * P],
-                        in_=scaled[:, g, b, :, :].rearrange("p r t -> p (r t)"),
+                        in_=scaled[:, b, g, :, :].rearrange("p r t -> p (r t)"),
                     )
 
         def first_stage(h):

@@ -49,28 +49,25 @@ def tile_littlebititqspeclinear_pa_kernel(
 
         ident_f32 = consts.tile([P, P], F32)
         make_identity(nc, ident_f32[:])
-        ident_bf16 = consts.tile([P, P], BF16)
-        make_identity(nc, ident_bf16[:])
 
-        word_rows = consts.tile([P, 2 * P], BF16)
-        nc.vector.memset(word_rows[:], 0.0)
-        first_row = 0
-        for vector in (v2, v2_R, v1, u2, v1_R, u2_R):
-            rows = vector.rearrange("o (c w) -> (o c) w", w=2 * P)
-            nc.sync.dma_start(out=word_rows[first_row : first_row + rows.shape[0], :], in_=rows)
-            first_row += rows.shape[0]
-        WORD_COLS = 2 * first_row
+        def load_vector_rows(vectors, name):
+            rows_tile = consts.tile([P, 2 * P], BF16, name=name)
+            nc.vector.memset(rows_tile[:], 0.0)
+            first_row = 0
+            for vector in vectors:
+                rows = vector.rearrange("(c w) -> c w", w=2 * P)
+                nc.sync.dma_start(out=rows_tile[first_row : first_row + rows.shape[0], :], in_=rows)
+                first_row += rows.shape[0]
+            return rows_tile
 
-        out_vec_rows = consts.tile([P, P], BF16)
-        nc.vector.memset(out_vec_rows[:], 0.0)
-        OUT_COLS = OUT // P
-        nc.gpsimd.dma_start(out=out_vec_rows[0:OUT_COLS, :], in_=u1.rearrange("o (c w) -> (o c) w", w=P))
-        nc.gpsimd.dma_start(
-            out=out_vec_rows[OUT_COLS : 2 * OUT_COLS, :], in_=u1_R.rearrange("o (c w) -> (o c) w", w=P)
-        )
-        nc.gpsimd.dma_start(
-            out=out_vec_rows[2 * OUT_COLS : 3 * OUT_COLS, :], in_=bias.rearrange("(c w) -> c w", w=P)
-        )
+        def transpose_vector_rows(rows_tile, n_rows, name):
+            bank = psum_x.tile([P, BANK], F32, tag="tx")
+            nc.tensor.transpose(bank[:, 0:P], rows_tile[:].bitcast(F32), ident_f32[:])
+            columns = consts.tile([P, 2 * n_rows], BF16, name=name)
+            nc.vector.tensor_copy(out=columns[:], in_=bank[:].bitcast(BF16)[:, 0 : 2 * n_rows])
+            return columns
+
+        v2_rows = load_vector_rows((v2[0, :], v2_R[0, :]), "v2_rows")
 
         weight_views = []
         for matrix in (V, V_R):
@@ -79,7 +76,7 @@ def tile_littlebititqspeclinear_pa_kernel(
                 weight_views.append(by_code[t // 2, t % 2])
         for og in range(O_GROUPS):
             for matrix in (U, U_R):
-                weight_views.append(matrix.rearrange("(g n p) s -> g p n s", n=O_TILES, p=P)[og])
+                weight_views.append(matrix.rearrange("(g c p e) s -> g p c (e s)", c=2, p=P, e=2)[og])
         x_views = x_rows.rearrange("(n p) k -> n p k", p=P)
 
         def load_weight(w):
@@ -87,7 +84,7 @@ def tile_littlebititqspeclinear_pa_kernel(
             if w < BRANCHES * S_TILES:
                 nc.sync.dma_start(out=raw[:], in_=weight_views[w])
             else:
-                nc.sync.dma_start(out=raw[:].rearrange("p (n s) -> p n s", n=O_TILES), in_=weight_views[w])
+                nc.sync.dma_start(out=raw[:].rearrange("p (c es) -> p c es", c=2), in_=weight_views[w])
             return raw
 
         def load_x(rt):
@@ -103,25 +100,28 @@ def tile_littlebititqspeclinear_pa_kernel(
             raw_x[j] = load_x(j)
             for w in range(WEIGHTS_PER_X_TILE * j + 1, WEIGHTS_PER_X_TILE * (j + 1)):
                 raw_w[w] = load_weight(w)
+            if j == 0:
+                late_rows = load_vector_rows(
+                    (v1[0, :], u2[0, :], v1_R[0, :], u2_R[0, :], u1[0, :], u1_R[0, :], bias), "late_rows"
+                )
         for j in range(X_TILES):
             raw_w[EARLY_WEIGHTS + j] = load_weight(EARLY_WEIGHTS + j)
             raw_x[X_TILES + j] = load_x(X_TILES + j)
 
-        word_bank = psum_x.tile([P, BANK], F32, tag="tx")
-        nc.tensor.transpose(word_bank[:, 0:P], word_rows[:].bitcast(F32), ident_f32[:])
-        k_vectors = consts.tile([P, WORD_COLS], BF16)
-        nc.vector.tensor_copy(out=k_vectors[:], in_=word_bank[:].bitcast(BF16)[:, 0:WORD_COLS])
-        V2_COLS = BRANCHES * PASSES * PACK
-        v1_and_u2 = k_vectors[:, V2_COLS:WORD_COLS].rearrange("p (b w t) -> p b w t", b=BRANCHES, w=2)
-        v1u2 = consts.tile([P, BRANCHES, PACK], F32)
-        nc.vector.tensor_tensor(out=v1u2[:], in0=v1_and_u2[:, :, 0, :], in1=v1_and_u2[:, :, 1, :], op=ALU.mult)
+        k_vectors = transpose_vector_rows(v2_rows, 2 * IN // (2 * P), "k_vectors")
 
-        out_vec_bank = psum_x.tile([P, P], BF16, tag="tx")
-        nc.tensor.transpose(out_vec_bank[:], out_vec_rows[:], ident_bf16[:])
-        o_vectors = consts.tile([P, 3, OUT_COLS], F32)
-        nc.vector.tensor_copy(
-            out=o_vectors[:].rearrange("p v c -> p (v c)"), in_=out_vec_bank[:, 0 : 3 * OUT_COLS]
-        )
+        def prepare_late_vectors():
+            H_COLS = SPLIT // P
+            O_COLS = OUT // P
+            columns = transpose_vector_rows(late_rows, (4 * SPLIT + 3 * OUT) // (2 * P), "late_columns")
+            v1_and_u2 = columns[:, 0 : 4 * H_COLS].rearrange("p (b w t) -> p b w t", b=BRANCHES, w=2)
+            nc.vector.tensor_tensor(out=v1u2[:], in0=v1_and_u2[:, :, 0, :], in1=v1_and_u2[:, :, 1, :], op=ALU.mult)
+            nc.vector.tensor_copy(
+                out=o_vectors[:].rearrange("p v c -> p (v c)"), in_=columns[:, 4 * H_COLS : 4 * H_COLS + 3 * O_COLS]
+            )
+
+        v1u2 = consts.tile([P, BRANCHES, PACK], F32)
+        o_vectors = consts.tile([P, 3, OUT // P], F32)
 
         v_codes = [keep.tile([P, S_TILES, K_PASS], U32, name="v_codes%d" % b, align_bytes=64) for b in range(2)]
         v_scales = [keep.tile([P, S_TILES, K_PASS], U8, name="v_scales%d" % b, align_bytes=64) for b in range(2)]
@@ -175,28 +175,23 @@ def tile_littlebititqspeclinear_pa_kernel(
         def prepare_x(rt):
             h, j = rt // X_TILES, rt % X_TILES
             banks = transpose_words(raw_x[rt], psum_x, "tx")
-            grouped = stage.tile([P, IN // 2], F32, tag="x_grouped")
-            by_pass = grouped[:].rearrange("p (g r u) -> p g r u", g=PASSES, u=2)
-            for i in range(2):
-                nc.vector.tensor_copy(
-                    out=by_pass[:, 2 * i : 2 * i + 2, :, :],
-                    in_=banks[i][:].rearrange("p (g u r) -> p g r u", g=2, u=2),
-                )
-            scaled = stage.tile([P, BRANCHES, PASSES, P, PACK], BF16, tag="scaled", align_bytes=64)
-            for b in range(BRANCHES):
-                factors = k_vectors[:, b * PASSES * PACK : (b + 1) * PASSES * PACK]
-                nc.vector.tensor_tensor(
-                    out=scaled[:, b, :, :, :],
-                    in0=grouped[:].bitcast(BF16).rearrange("p (g r t) -> p g r t", g=PASSES, t=PACK),
-                    in1=factors.rearrange("p (g t) -> p g t", g=PASSES).unsqueeze(2).to_broadcast([P, PASSES, P, PACK]),
-                    op=ALU.mult,
-                )
-            for b in range(BRANCHES):
-                for g in range(PASSES):
+            scaled = stage.tile([P, PASSES, BRANCHES, P, PACK], BF16, tag="scaled", align_bytes=64)
+            for g in range(PASSES):
+                for b in range(BRANCHES):
+                    first = (b * PASSES + g) * PACK
+                    factors = k_vectors[:, first : first + PACK].rearrange("p (u e) -> p u e", u=2)
+                    nc.vector.tensor_tensor(
+                        out=scaled[:, g, b, :, :].rearrange("p r (u e) -> p r u e", u=2),
+                        in0=unit_by_row(banks, g),
+                        in1=factors.unsqueeze(1).to_broadcast([P, P, 2, 2]),
+                        op=ALU.mult,
+                    )
+            for g in range(PASSES):
+                for b in range(BRANCHES):
                     nc.vector.quantize_mx(
                         out=x_codes[b, h][:, g, j * P : (j + 1) * P].bitcast(FP8X4),
                         scales=x_scales[b, h][:, g, j * P : (j + 1) * P],
-                        in_=scaled[:, b, g, :, :].rearrange("p r t -> p (r t)"),
+                        in_=scaled[:, g, b, :, :].rearrange("p r t -> p (r t)"),
                     )
 
         def first_stage(h):
@@ -266,10 +261,12 @@ def tile_littlebititqspeclinear_pa_kernel(
                         bank[:, ol * P : (ol + 1) * P], total[:, ol, j * P : (j + 1) * P], ident_f32[:]
                     )
                 result = stage.tile([P, BANK], F32, tag="result", bufs=4)
+                in_order = bank[:].rearrange("r (c e p) -> r c p e", c=2, e=2)
+                by_pair = result[:].rearrange("r (c p e) -> r c p e", c=2, e=2)
                 if h == HALVES - 1 and j % 2 == 1:
-                    nc.vector.tensor_copy(out=result[:], in_=bank[:])
+                    nc.vector.tensor_copy(out=by_pair, in_=in_order)
                 else:
-                    nc.scalar.copy(out=result[:], in_=bank[:])
+                    nc.scalar.copy(out=by_pair, in_=in_order)
                 r0 = h * BANK + j * P
                 nc.sync.dma_start(out=out_rows[r0 : r0 + P, og * BANK : (og + 1) * BANK], in_=result[:])
 
@@ -277,6 +274,7 @@ def tile_littlebititqspeclinear_pa_kernel(
             prepare_x(j)
             for w in range(WEIGHTS_PER_X_TILE * j, WEIGHTS_PER_X_TILE * (j + 1)):
                 prepare_weight(w)
+        prepare_late_vectors()
         first_stage(0)
         for j in range(X_TILES):
             prepare_weight(EARLY_WEIGHTS + j)

@@ -47,16 +47,13 @@ def tile_littlebititqspeclinear_pa_kernel(
         psum_x = ctx.enter_context(tc.psum_pool(name="psum_x", bufs=2))
         psum_acc = ctx.enter_context(tc.psum_pool(name="psum_acc", bufs=4))
 
-        ident_f32 = consts.tile([P, P], F32)
-        make_identity(nc, ident_f32[:])
-
         def load_vector_rows(vectors, name):
             rows_tile = consts.tile([P, 2 * P], BF16, name=name)
             nc.vector.memset(rows_tile[:], 0.0)
             first_row = 0
             for vector in vectors:
                 rows = vector.rearrange("(c w) -> c w", w=2 * P)
-                nc.sync.dma_start(out=rows_tile[first_row : first_row + rows.shape[0], :], in_=rows)
+                nc.gpsimd.dma_start(out=rows_tile[first_row : first_row + rows.shape[0], :], in_=rows)
                 first_row += rows.shape[0]
             return rows_tile
 
@@ -68,6 +65,11 @@ def tile_littlebititqspeclinear_pa_kernel(
             return columns
 
         v2_rows = load_vector_rows((v2[0, :], v2_R[0, :]), "v2_rows")
+        ident_f32 = consts.tile([P, P], F32)
+        make_identity(nc, ident_f32[:])
+        late_rows = load_vector_rows(
+            (v1[0, :], u2[0, :], v1_R[0, :], u2_R[0, :], u1[0, :], u1_R[0, :], bias), "late_rows"
+        )
 
         weight_views = []
         for matrix in (V, V_R):
@@ -100,10 +102,6 @@ def tile_littlebititqspeclinear_pa_kernel(
             raw_x[j] = load_x(j)
             for w in range(WEIGHTS_PER_X_TILE * j + 1, WEIGHTS_PER_X_TILE * (j + 1)):
                 raw_w[w] = load_weight(w)
-            if j == 0:
-                late_rows = load_vector_rows(
-                    (v1[0, :], u2[0, :], v1_R[0, :], u2_R[0, :], u1[0, :], u1_R[0, :], bias), "late_rows"
-                )
         for j in range(X_TILES):
             raw_w[EARLY_WEIGHTS + j] = load_weight(EARLY_WEIGHTS + j)
             raw_x[X_TILES + j] = load_x(X_TILES + j)

@@ -25,8 +25,8 @@ X_TILES = BANK // P
 S_TILES = SPLIT // P
 O_GROUPS = OUT // BANK
 O_TILES = BANK // P
-RAW_SLOTS = 14
-WEIGHTS_PER_X_TILE = 3
+RAW_SLOTS = 12
+WEIGHTS_PER_X_TILE = 4
 
 FLOPS = 2 * BRANCHES * (ROWS * IN * SPLIT + ROWS * SPLIT * OUT)
 
@@ -45,30 +45,32 @@ def tile_littlebititqspeclinear_pa_kernel(
         stage = ctx.enter_context(tc.tile_pool(name="stage", bufs=2))
         psum_w = ctx.enter_context(tc.psum_pool(name="psum_w", bufs=2))
         psum_x = ctx.enter_context(tc.psum_pool(name="psum_x", bufs=2))
-        psum_acc = ctx.enter_context(tc.psum_pool(name="psum_acc", bufs=4))
+        psum_s = ctx.enter_context(tc.psum_pool(name="psum_s", bufs=2))
+        psum_v = ctx.enter_context(tc.psum_pool(name="psum_v", bufs=2))
 
-        def load_vector_rows(vectors, name):
-            rows_tile = consts.tile([P, 2 * P], BF16, name=name)
-            nc.vector.memset(rows_tile[:], 0.0)
-            first_row = 0
-            for vector in vectors:
-                rows = vector.rearrange("(c w) -> c w", w=2 * P)
-                nc.gpsimd.dma_start(out=rows_tile[first_row : first_row + rows.shape[0], :], in_=rows)
-                first_row += rows.shape[0]
-            return rows_tile
-
-        def transpose_vector_rows(rows_tile, n_rows, name):
-            bank = psum_x.tile([P, BANK], F32, tag="tx")
-            nc.tensor.transpose(bank[:, 0:P], rows_tile[:].bitcast(F32), ident_f32[:])
-            columns = consts.tile([P, 2 * n_rows], BF16, name=name)
-            nc.vector.tensor_copy(out=columns[:], in_=bank[:].bitcast(BF16)[:, 0 : 2 * n_rows])
-            return columns
-
-        v2_rows = load_vector_rows((v2[0, :], v2_R[0, :]), "v2_rows")
         ident_f32 = consts.tile([P, P], F32)
         make_identity(nc, ident_f32[:])
-        late_rows = load_vector_rows(
-            (v1[0, :], u2[0, :], v1_R[0, :], u2_R[0, :], u1[0, :], u1_R[0, :], bias), "late_rows"
+        ident_bf16 = consts.tile([P, P], BF16)
+        make_identity(nc, ident_bf16[:])
+
+        word_rows = consts.tile([P, 2 * P], BF16)
+        nc.vector.memset(word_rows[:], 0.0)
+        first_row = 0
+        for vector in (v2, v2_R, v1, u2, v1_R, u2_R):
+            rows = vector.rearrange("o (c w) -> (o c) w", w=2 * P)
+            nc.sync.dma_start(out=word_rows[first_row : first_row + rows.shape[0], :], in_=rows)
+            first_row += rows.shape[0]
+        WORD_COLS = 2 * first_row
+
+        out_vec_rows = consts.tile([P, P], BF16)
+        nc.vector.memset(out_vec_rows[:], 0.0)
+        OUT_COLS = OUT // P
+        nc.gpsimd.dma_start(out=out_vec_rows[0:OUT_COLS, :], in_=u1.rearrange("o (c w) -> (o c) w", w=P))
+        nc.gpsimd.dma_start(
+            out=out_vec_rows[OUT_COLS : 2 * OUT_COLS, :], in_=u1_R.rearrange("o (c w) -> (o c) w", w=P)
+        )
+        nc.gpsimd.dma_start(
+            out=out_vec_rows[2 * OUT_COLS : 3 * OUT_COLS, :], in_=bias.rearrange("(c w) -> c w", w=P)
         )
 
         weight_views = []
@@ -78,7 +80,7 @@ def tile_littlebititqspeclinear_pa_kernel(
                 weight_views.append(by_code[t // 2, t % 2])
         for og in range(O_GROUPS):
             for matrix in (U, U_R):
-                weight_views.append(matrix.rearrange("(g c p e) s -> g p c (e s)", c=2, p=P, e=2)[og])
+                weight_views.append(matrix.rearrange("(g n p) s -> g p n s", n=O_TILES, p=P)[og])
         x_views = x_rows.rearrange("(n p) k -> n p k", p=P)
 
         def load_weight(w):
@@ -86,7 +88,7 @@ def tile_littlebititqspeclinear_pa_kernel(
             if w < BRANCHES * S_TILES:
                 nc.sync.dma_start(out=raw[:], in_=weight_views[w])
             else:
-                nc.sync.dma_start(out=raw[:].rearrange("p (c es) -> p c es", c=2), in_=weight_views[w])
+                nc.sync.dma_start(out=raw[:].rearrange("p (n s) -> p n s", n=O_TILES), in_=weight_views[w])
             return raw
 
         def load_x(rt):
@@ -96,30 +98,29 @@ def tile_littlebititqspeclinear_pa_kernel(
 
         raw_w = {}
         raw_x = {}
-        EARLY_WEIGHTS = WEIGHTS_PER_X_TILE * X_TILES
         for j in range(X_TILES):
             raw_w[WEIGHTS_PER_X_TILE * j] = load_weight(WEIGHTS_PER_X_TILE * j)
             raw_x[j] = load_x(j)
             for w in range(WEIGHTS_PER_X_TILE * j + 1, WEIGHTS_PER_X_TILE * (j + 1)):
                 raw_w[w] = load_weight(w)
         for j in range(X_TILES):
-            raw_w[EARLY_WEIGHTS + j] = load_weight(EARLY_WEIGHTS + j)
             raw_x[X_TILES + j] = load_x(X_TILES + j)
 
-        k_vectors = transpose_vector_rows(v2_rows, 2 * IN // (2 * P), "k_vectors")
-
-        def prepare_late_vectors():
-            H_COLS = SPLIT // P
-            O_COLS = OUT // P
-            columns = transpose_vector_rows(late_rows, (4 * SPLIT + 3 * OUT) // (2 * P), "late_columns")
-            v1_and_u2 = columns[:, 0 : 4 * H_COLS].rearrange("p (b w t) -> p b w t", b=BRANCHES, w=2)
-            nc.vector.tensor_tensor(out=v1u2[:], in0=v1_and_u2[:, :, 0, :], in1=v1_and_u2[:, :, 1, :], op=ALU.mult)
-            nc.vector.tensor_copy(
-                out=o_vectors[:].rearrange("p v c -> p (v c)"), in_=columns[:, 4 * H_COLS : 4 * H_COLS + 3 * O_COLS]
-            )
-
+        word_bank = psum_x.tile([P, BANK], F32, tag="tx")
+        nc.tensor.transpose(word_bank[:, 0:P], word_rows[:].bitcast(F32), ident_f32[:])
+        k_vectors = consts.tile([P, WORD_COLS], BF16)
+        nc.vector.tensor_copy(out=k_vectors[:], in_=word_bank[:].bitcast(BF16)[:, 0:WORD_COLS])
+        V2_COLS = BRANCHES * PASSES * PACK
+        v1_and_u2 = k_vectors[:, V2_COLS:WORD_COLS].rearrange("p (b w t) -> p b w t", b=BRANCHES, w=2)
         v1u2 = consts.tile([P, BRANCHES, PACK], F32)
-        o_vectors = consts.tile([P, 3, OUT // P], F32)
+        nc.vector.tensor_tensor(out=v1u2[:], in0=v1_and_u2[:, :, 0, :], in1=v1_and_u2[:, :, 1, :], op=ALU.mult)
+
+        out_vec_bank = psum_x.tile([P, P], BF16, tag="tx")
+        nc.tensor.transpose(out_vec_bank[:], out_vec_rows[:], ident_bf16[:])
+        o_vectors = consts.tile([P, 3, OUT_COLS], F32)
+        nc.vector.tensor_copy(
+            out=o_vectors[:].rearrange("p v c -> p (v c)"), in_=out_vec_bank[:, 0 : 3 * OUT_COLS]
+        )
 
         v_codes = [keep.tile([P, S_TILES, K_PASS], U32, name="v_codes%d" % b, align_bytes=64) for b in range(2)]
         v_scales = [keep.tile([P, S_TILES, K_PASS], U8, name="v_scales%d" % b, align_bytes=64) for b in range(2)]
@@ -153,7 +154,7 @@ def tile_littlebititqspeclinear_pa_kernel(
 
         def prepare_weight(w):
             banks = transpose_words(raw_w[w], psum_w, "tw")
-            signs = stage.tile([P, UNITS, P, PACK], BF16, tag="signs", align_bytes=64)
+            signs = stage.tile([P, UNITS, P, PACK], BF16, tag="signs", bufs=3, align_bytes=64)
             for n in range(UNITS):
                 nc.scalar.activation(
                     out=signs[:, n, :, :].rearrange("p r (u e) -> p r u e", u=2),
@@ -196,7 +197,7 @@ def tile_littlebititqspeclinear_pa_kernel(
             for b in range(BRANCHES):
                 planes = stage.tile([P, S_TILES, BANK], BF16, tag="planes")
                 for t in range(S_TILES):
-                    acc = psum_acc.tile([P, BANK], F32, tag="acc")
+                    acc = psum_s.tile([P, BANK], F32, tag="acc_s")
                     for g in range(PASSES):
                         nc.tensor.matmul_mx(
                             out=acc[:],
@@ -220,51 +221,58 @@ def tile_littlebititqspeclinear_pa_kernel(
                 )
 
         def second_stage(h, og):
-            total = stage.tile([P, O_TILES, BANK], F32, tag="total")
-            for ol in range(O_TILES):
+            total = stage.tile([P, O_TILES, BANK], F32, tag="total", bufs=3)
+
+            def product(pool, tag, b, ol):
+                acc = pool.tile([P, BANK], F32, tag=tag)
+                nc.tensor.matmul_mx(
+                    out=acc[:],
+                    lhsT=u_codes[b][:, og, ol * P : (ol + 1) * P].bitcast(FP8X4),
+                    lhsT_scale=u_scales[b][:, og, ol * P : (ol + 1) * P],
+                    rhs=h_codes[b, h][:].bitcast(FP8X4),
+                    rhs_scale=h_scales[b, h][:],
+                    start=True,
+                    stop=True,
+                )
+                return acc
+
+            def main_branch(ol):
                 ot = og * O_TILES + ol
-                products = []
-                for b in range(BRANCHES):
-                    acc = psum_acc.tile([P, BANK], F32, tag="acc")
-                    nc.tensor.matmul_mx(
-                        out=acc[:],
-                        lhsT=u_codes[b][:, og, ol * P : (ol + 1) * P].bitcast(FP8X4),
-                        lhsT_scale=u_scales[b][:, og, ol * P : (ol + 1) * P],
-                        rhs=h_codes[b, h][:].bitcast(FP8X4),
-                        rhs_scale=h_scales[b, h][:],
-                        start=True,
-                        stop=True,
-                    )
-                    products.append(acc)
-                main = stage.tile([P, BANK], F32, tag="main")
                 nc.scalar.activation(
-                    out=main[:],
-                    in_=products[0][:],
+                    out=total[:, ol, :],
+                    in_=product(psum_s, "acc_s", 0, ol)[:],
                     func=ACT.Identity,
                     scale=o_vectors[:, 0, ot : ot + 1],
                     bias=o_vectors[:, 2, ot : ot + 1],
                 )
+
+            def add_residual_branch(ol):
+                ot = og * O_TILES + ol
                 nc.vector.scalar_tensor_tensor(
                     out=total[:, ol, :],
-                    in0=products[1][:],
+                    in0=product(psum_v, "acc_v", 1, ol)[:],
                     scalar=o_vectors[:, 1, ot : ot + 1],
-                    in1=main[:],
+                    in1=total[:, ol, :],
                     op0=ALU.mult,
                     op1=ALU.add,
                 )
+
+            main_branch(0)
+            for ol in range(O_TILES):
+                if ol + 1 < O_TILES:
+                    main_branch(ol + 1)
+                add_residual_branch(ol)
             for j in range(X_TILES):
                 bank = psum_w.tile([P, BANK], F32, tag="tw")
                 for ol in range(O_TILES):
                     nc.tensor.transpose(
                         bank[:, ol * P : (ol + 1) * P], total[:, ol, j * P : (j + 1) * P], ident_f32[:]
                     )
-                result = stage.tile([P, BANK], F32, tag="result", bufs=4)
-                in_order = bank[:].rearrange("r (c e p) -> r c p e", c=2, e=2)
-                by_pair = result[:].rearrange("r (c p e) -> r c p e", c=2, e=2)
+                result = stage.tile([P, BANK], F32, tag="result", bufs=6)
                 if h == HALVES - 1 and j % 2 == 1:
-                    nc.vector.tensor_copy(out=by_pair, in_=in_order)
+                    nc.vector.tensor_copy(out=result[:], in_=bank[:])
                 else:
-                    nc.scalar.copy(out=by_pair, in_=in_order)
+                    nc.scalar.copy(out=result[:], in_=bank[:])
                 r0 = h * BANK + j * P
                 nc.sync.dma_start(out=out_rows[r0 : r0 + P, og * BANK : (og + 1) * BANK], in_=result[:])
 
@@ -272,10 +280,8 @@ def tile_littlebititqspeclinear_pa_kernel(
             prepare_x(j)
             for w in range(WEIGHTS_PER_X_TILE * j, WEIGHTS_PER_X_TILE * (j + 1)):
                 prepare_weight(w)
-        prepare_late_vectors()
         first_stage(0)
         for j in range(X_TILES):
-            prepare_weight(EARLY_WEIGHTS + j)
             prepare_x(X_TILES + j)
             second_stage(0, j)
         first_stage(1)

@@ -25,7 +25,7 @@ X_TILES = BANK // P
 S_TILES = SPLIT // P
 O_GROUPS = OUT // BANK
 O_TILES = BANK // P
-RAW_SLOTS = 12
+RAW_SLOTS = 10
 WEIGHTS_PER_X_TILE = 4
 
 FLOPS = 2 * BRANCHES * (ROWS * IN * SPLIT + ROWS * SPLIT * OUT)
@@ -171,26 +171,37 @@ def tile_littlebititqspeclinear_pa_kernel(
                 out=codes.bitcast(FP8X4), scales=scales, in_=signs[:].rearrange("p n r t -> p (n r t)")
             )
 
+        factors = consts.tile([P, BRANCHES, IN], BF16)
+        for b in range(BRANCHES):
+            one_row = k_vectors[:, b * PASSES * PACK : (b + 1) * PASSES * PACK].rearrange("p (g t) -> p g t", g=PASSES)
+            every_row = one_row.unsqueeze(2).to_broadcast([P, PASSES, P, PACK])
+            repeated = factors[:, b, :].rearrange("p (g r t) -> p g r t", g=PASSES, t=PACK)
+            if b == 0:
+                nc.vector.tensor_copy(out=repeated, in_=every_row)
+            else:
+                nc.scalar.copy(out=repeated, in_=every_row)
+
         def prepare_x(rt):
             h, j = rt // X_TILES, rt % X_TILES
             banks = transpose_words(raw_x[rt], psum_x, "tx")
-            scaled = stage.tile([P, PASSES, BRANCHES, P, PACK], BF16, tag="scaled", align_bytes=64)
-            for g in range(PASSES):
-                for b in range(BRANCHES):
-                    first = (b * PASSES + g) * PACK
-                    factors = k_vectors[:, first : first + PACK].rearrange("p (u e) -> p u e", u=2)
-                    nc.vector.tensor_tensor(
-                        out=scaled[:, g, b, :, :].rearrange("p r (u e) -> p r u e", u=2),
-                        in0=unit_by_row(banks, g),
-                        in1=factors.unsqueeze(1).to_broadcast([P, P, 2, 2]),
-                        op=ALU.mult,
-                    )
-            for g in range(PASSES):
-                for b in range(BRANCHES):
+            grouped = stage.tile([P, IN // 2], F32, tag="x_grouped")
+            by_pass = grouped[:].rearrange("p (g r u) -> p g r u", g=PASSES, u=2)
+            for i in range(2):
+                nc.vector.tensor_copy(
+                    out=by_pass[:, 2 * i : 2 * i + 2, :, :],
+                    in_=banks[i][:].rearrange("p (g u r) -> p g r u", g=2, u=2),
+                )
+            scaled = stage.tile([P, BRANCHES, IN], BF16, tag="scaled", align_bytes=64)
+            for b in range(BRANCHES):
+                nc.vector.tensor_tensor(
+                    out=scaled[:, b, :], in0=grouped[:].bitcast(BF16), in1=factors[:, b, :], op=ALU.mult
+                )
+            for b in range(BRANCHES):
+                for g in range(PASSES):
                     nc.vector.quantize_mx(
                         out=x_codes[b, h][:, g, j * P : (j + 1) * P].bitcast(FP8X4),
                         scales=x_scales[b, h][:, g, j * P : (j + 1) * P],
-                        in_=scaled[:, g, b, :, :].rearrange("p r t -> p (r t)"),
+                        in_=scaled[:, b, g * K_PASS : (g + 1) * K_PASS],
                     )
 
         def first_stage(h):
@@ -268,7 +279,7 @@ def tile_littlebititqspeclinear_pa_kernel(
                     nc.tensor.transpose(
                         bank[:, ol * P : (ol + 1) * P], total[:, ol, j * P : (j + 1) * P], ident_f32[:]
                     )
-                result = stage.tile([P, BANK], F32, tag="result", bufs=6)
+                result = stage.tile([P, BANK], F32, tag="result", bufs=4)
                 if h == HALVES - 1 and j % 2 == 1:
                     nc.vector.tensor_copy(out=result[:], in_=bank[:])
                 else:

@@ -22,11 +22,14 @@ PASSES = IN // K_PASS
 UNITS = 4
 HALVES = ROWS // BANK
 X_TILES = BANK // P
+PAIR = 2 * P
+PAIRS = BANK // PAIR
 S_TILES = SPLIT // P
 O_GROUPS = OUT // BANK
 O_TILES = BANK // P
-RAW_SLOTS = 10
-WEIGHTS_PER_X_TILE = 4
+RAW_W_SLOTS = 8
+RAW_X_SLOTS = 2
+WEIGHTS_PER_PAIR = 8
 
 FLOPS = 2 * BRANCHES * (ROWS * IN * SPLIT + ROWS * SPLIT * OUT)
 
@@ -41,7 +44,8 @@ def tile_littlebititqspeclinear_pa_kernel(
     with ExitStack() as ctx:
         consts = ctx.enter_context(tc.tile_pool(name="consts", bufs=1))
         keep = ctx.enter_context(tc.tile_pool(name="keep", bufs=1))
-        raws = ctx.enter_context(tc.tile_pool(name="raws", bufs=RAW_SLOTS))
+        raws_w = ctx.enter_context(tc.tile_pool(name="raws_w", bufs=RAW_W_SLOTS))
+        raws_x = ctx.enter_context(tc.tile_pool(name="raws_x", bufs=RAW_X_SLOTS))
         stage = ctx.enter_context(tc.tile_pool(name="stage", bufs=2))
         psum_w = ctx.enter_context(tc.psum_pool(name="psum_w", bufs=2))
         psum_x = ctx.enter_context(tc.psum_pool(name="psum_x", bufs=2))
@@ -81,30 +85,30 @@ def tile_littlebititqspeclinear_pa_kernel(
         for og in range(O_GROUPS):
             for matrix in (U, U_R):
                 weight_views.append(matrix.rearrange("(g n p) s -> g p n s", n=O_TILES, p=P)[og])
-        x_views = x_rows.rearrange("(n p) k -> n p k", p=P)
+        x_views = x_rows.rearrange("(n i p) k -> n p i k", i=2, p=P)
 
         def load_weight(w):
-            raw = raws.tile([P, IN], BF16, tag="raw", name="raw_w%d" % w)
+            raw = raws_w.tile([P, IN], BF16, tag="raw_w", name="raw_w%d" % w)
             if w < BRANCHES * S_TILES:
                 nc.sync.dma_start(out=raw[:], in_=weight_views[w])
             else:
                 nc.sync.dma_start(out=raw[:].rearrange("p (n s) -> p n s", n=O_TILES), in_=weight_views[w])
             return raw
 
-        def load_x(rt):
-            raw = raws.tile([P, IN], BF16, tag="raw", name="raw_x%d" % rt)
-            nc.sync.dma_start(out=raw[:], in_=x_views[rt])
+        def load_x(pair):
+            raw = raws_x.tile([P, 2 * IN], BF16, tag="raw_x", name="raw_x%d" % pair)
+            nc.sync.dma_start(out=raw[:].rearrange("p (i k) -> p i k", i=2), in_=x_views[pair])
             return raw
 
         raw_w = {}
         raw_x = {}
-        for j in range(X_TILES):
-            raw_w[WEIGHTS_PER_X_TILE * j] = load_weight(WEIGHTS_PER_X_TILE * j)
+        for j in range(PAIRS):
+            raw_w[WEIGHTS_PER_PAIR * j] = load_weight(WEIGHTS_PER_PAIR * j)
             raw_x[j] = load_x(j)
-            for w in range(WEIGHTS_PER_X_TILE * j + 1, WEIGHTS_PER_X_TILE * (j + 1)):
+            for w in range(WEIGHTS_PER_PAIR * j + 1, WEIGHTS_PER_PAIR * (j + 1)):
                 raw_w[w] = load_weight(w)
-        for j in range(X_TILES):
-            raw_x[X_TILES + j] = load_x(X_TILES + j)
+        for j in range(PAIRS):
+            raw_x[PAIRS + j] = load_x(PAIRS + j)
 
         word_bank = psum_x.tile([P, BANK], F32, tag="tx")
         nc.tensor.transpose(word_bank[:, 0:P], word_rows[:].bitcast(F32), ident_f32[:])
@@ -171,38 +175,37 @@ def tile_littlebititqspeclinear_pa_kernel(
                 out=codes.bitcast(FP8X4), scales=scales, in_=signs[:].rearrange("p n r t -> p (n r t)")
             )
 
-        factors = consts.tile([P, BRANCHES, IN], BF16)
-        for b in range(BRANCHES):
-            one_row = k_vectors[:, b * PASSES * PACK : (b + 1) * PASSES * PACK].rearrange("p (g t) -> p g t", g=PASSES)
-            every_row = one_row.unsqueeze(2).to_broadcast([P, PASSES, P, PACK])
-            repeated = factors[:, b, :].rearrange("p (g r t) -> p g r t", g=PASSES, t=PACK)
-            if b == 0:
-                nc.vector.tensor_copy(out=repeated, in_=every_row)
-            else:
-                nc.scalar.copy(out=repeated, in_=every_row)
-
-        def prepare_x(rt):
-            h, j = rt // X_TILES, rt % X_TILES
-            banks = transpose_words(raw_x[rt], psum_x, "tx")
-            grouped = stage.tile([P, IN // 2], F32, tag="x_grouped")
-            by_pass = grouped[:].rearrange("p (g r u) -> p g r u", g=PASSES, u=2)
-            for i in range(2):
-                nc.vector.tensor_copy(
-                    out=by_pass[:, 2 * i : 2 * i + 2, :, :],
-                    in_=banks[i][:].rearrange("p (g u r) -> p g r u", g=2, u=2),
-                )
-            scaled = stage.tile([P, BRANCHES, IN], BF16, tag="scaled", align_bytes=64)
-            for b in range(BRANCHES):
-                nc.vector.tensor_tensor(
-                    out=scaled[:, b, :], in0=grouped[:].bitcast(BF16), in1=factors[:, b, :], op=ALU.mult
-                )
-            for b in range(BRANCHES):
-                for g in range(PASSES):
-                    nc.vector.quantize_mx(
-                        out=x_codes[b, h][:, g, j * P : (j + 1) * P].bitcast(FP8X4),
-                        scales=x_scales[b, h][:, g, j * P : (j + 1) * P],
-                        in_=scaled[:, b, g * K_PASS : (g + 1) * K_PASS],
-                    )
+        def prepare_x(pair):
+            h, j = pair // PAIRS, pair % PAIRS
+            words = raw_x[pair][:].bitcast(F32)
+            waiting = []
+            for g in range(PASSES + 1):
+                if g < PASSES:
+                    bank = psum_x.tile([P, BANK], F32, tag="tx")
+                    for u in range(2):
+                        for i in range(2):
+                            first = i * (IN // 2) + (2 * g + u) * P
+                            nc.tensor.transpose(
+                                bank[:, (2 * u + i) * P : (2 * u + i + 1) * P], words[:, first : first + P], ident_f32[:]
+                            )
+                    scaled = stage.tile([P, BRANCHES, PAIR, PACK], BF16, tag="scaled", bufs=4, align_bytes=64)
+                    for b in range(BRANCHES):
+                        first = (b * PASSES + g) * PACK
+                        factors = k_vectors[:, first : first + PACK].rearrange("p (u e) -> p u e", u=2)
+                        nc.vector.tensor_tensor(
+                            out=scaled[:, b, :, :].rearrange("p r (u e) -> p r u e", u=2),
+                            in0=bank[:].bitcast(BF16).rearrange("p (u r e) -> p r u e", u=2, e=2),
+                            in1=factors.unsqueeze(1).to_broadcast([P, PAIR, 2, 2]),
+                            op=ALU.mult,
+                        )
+                for ready_g, ready in waiting:
+                    for b in range(BRANCHES):
+                        nc.vector.quantize_mx(
+                            out=x_codes[b, h][:, ready_g, j * PAIR : (j + 1) * PAIR].bitcast(FP8X4),
+                            scales=x_scales[b, h][:, ready_g, j * PAIR : (j + 1) * PAIR],
+                            in_=ready[:, b, :, :].rearrange("p r t -> p (r t)"),
+                        )
+                waiting = [(g, scaled)] if g < PASSES else []
 
         def first_stage(h):
             for b in range(BRANCHES):
@@ -279,7 +282,7 @@ def tile_littlebititqspeclinear_pa_kernel(
                     nc.tensor.transpose(
                         bank[:, ol * P : (ol + 1) * P], total[:, ol, j * P : (j + 1) * P], ident_f32[:]
                     )
-                result = stage.tile([P, BANK], F32, tag="result", bufs=4)
+                result = stage.tile([P, BANK], F32, tag="result", bufs=6)
                 if h == HALVES - 1 and j % 2 == 1:
                     nc.vector.tensor_copy(out=result[:], in_=bank[:])
                 else:
@@ -287,14 +290,15 @@ def tile_littlebititqspeclinear_pa_kernel(
                 r0 = h * BANK + j * P
                 nc.sync.dma_start(out=out_rows[r0 : r0 + P, og * BANK : (og + 1) * BANK], in_=result[:])
 
-        for j in range(X_TILES):
+        for j in range(PAIRS):
             prepare_x(j)
-            for w in range(WEIGHTS_PER_X_TILE * j, WEIGHTS_PER_X_TILE * (j + 1)):
+            for w in range(WEIGHTS_PER_PAIR * j, WEIGHTS_PER_PAIR * (j + 1)):
                 prepare_weight(w)
         first_stage(0)
-        for j in range(X_TILES):
-            prepare_x(X_TILES + j)
-            second_stage(0, j)
+        for j in range(PAIRS):
+            prepare_x(PAIRS + j)
+            second_stage(0, 2 * j)
+            second_stage(0, 2 * j + 1)
         first_stage(1)
         for og in range(O_GROUPS):
             second_stage(1, og)

@@ -27,9 +27,11 @@ PAIRS = BANK // PAIR
 S_TILES = SPLIT // P
 O_GROUPS = OUT // BANK
 O_TILES = BANK // P
+V_WEIGHTS = BRANCHES * S_TILES
+WEIGHTS = V_WEIGHTS + BRANCHES * O_GROUPS
 RAW_W_SLOTS = 8
 RAW_X_SLOTS = 2
-WEIGHTS_PER_PAIR = 8
+BANKS = 8
 
 FLOPS = 2 * BRANCHES * (ROWS * IN * SPLIT + ROWS * SPLIT * OUT)
 
@@ -47,10 +49,7 @@ def tile_littlebititqspeclinear_pa_kernel(
         raws_w = ctx.enter_context(tc.tile_pool(name="raws_w", bufs=RAW_W_SLOTS))
         raws_x = ctx.enter_context(tc.tile_pool(name="raws_x", bufs=RAW_X_SLOTS))
         stage = ctx.enter_context(tc.tile_pool(name="stage", bufs=2))
-        psum_w = ctx.enter_context(tc.psum_pool(name="psum_w", bufs=2))
-        psum_x = ctx.enter_context(tc.psum_pool(name="psum_x", bufs=2))
-        psum_s = ctx.enter_context(tc.psum_pool(name="psum_s", bufs=2))
-        psum_v = ctx.enter_context(tc.psum_pool(name="psum_v", bufs=2))
+        psum = ctx.enter_context(tc.psum_pool(name="psum", bufs=BANKS))
 
         ident_f32 = consts.tile([P, P], F32)
         make_identity(nc, ident_f32[:])
@@ -100,31 +99,15 @@ def tile_littlebititqspeclinear_pa_kernel(
             nc.sync.dma_start(out=raw[:].rearrange("p (i k) -> p i k", i=2), in_=x_views[pair])
             return raw
 
+        ctx.enter_context(tc.manual_schedule())
         raw_w = {}
         raw_x = {}
-        for j in range(PAIRS):
-            raw_w[WEIGHTS_PER_PAIR * j] = load_weight(WEIGHTS_PER_PAIR * j)
-            raw_x[j] = load_x(j)
-            for w in range(WEIGHTS_PER_PAIR * j + 1, WEIGHTS_PER_PAIR * (j + 1)):
+        for pair, before in enumerate((1, 4, 10, 12)):
+            for w in range(len(raw_w), before):
                 raw_w[w] = load_weight(w)
-        for j in range(PAIRS):
-            raw_x[PAIRS + j] = load_x(PAIRS + j)
-
-        word_bank = psum_x.tile([P, BANK], F32, tag="tx")
-        nc.tensor.transpose(word_bank[:, 0:P], word_rows[:].bitcast(F32), ident_f32[:])
-        k_vectors = consts.tile([P, WORD_COLS], BF16)
-        nc.vector.tensor_copy(out=k_vectors[:], in_=word_bank[:].bitcast(BF16)[:, 0:WORD_COLS])
-        V2_COLS = BRANCHES * PASSES * PACK
-        v1_and_u2 = k_vectors[:, V2_COLS:WORD_COLS].rearrange("p (b w t) -> p b w t", b=BRANCHES, w=2)
-        v1u2 = consts.tile([P, BRANCHES, PACK], F32)
-        nc.vector.tensor_tensor(out=v1u2[:], in0=v1_and_u2[:, :, 0, :], in1=v1_and_u2[:, :, 1, :], op=ALU.mult)
-
-        out_vec_bank = psum_x.tile([P, P], BF16, tag="tx")
-        nc.tensor.transpose(out_vec_bank[:], out_vec_rows[:], ident_bf16[:])
-        o_vectors = consts.tile([P, 3, OUT_COLS], F32)
-        nc.vector.tensor_copy(
-            out=o_vectors[:].rearrange("p v c -> p (v c)"), in_=out_vec_bank[:, 0 : 3 * OUT_COLS]
-        )
+            raw_x[pair] = load_x(pair)
+        for w in range(len(raw_w), WEIGHTS):
+            raw_w[w] = load_weight(w)
 
         v_codes = [keep.tile([P, S_TILES, K_PASS], U32, name="v_codes%d" % b, align_bytes=64) for b in range(2)]
         v_scales = [keep.tile([P, S_TILES, K_PASS], U8, name="v_scales%d" % b, align_bytes=64) for b in range(2)]
@@ -141,11 +124,11 @@ def tile_littlebititqspeclinear_pa_kernel(
                 h_codes[b, h] = keep.tile([P, BANK], U32, name="h_codes%d%d" % (b, h), align_bytes=64)
                 h_scales[b, h] = keep.tile([P, BANK], U8, name="h_scales%d%d" % (b, h), align_bytes=64)
 
-        def transpose_words(raw, pool, tag):
+        def transpose_words(raw):
             words = raw[:].bitcast(F32)
             banks = []
             for i in range(2):
-                bank = pool.tile([P, BANK], F32, tag=tag)
+                bank = psum.tile([P, BANK], F32, tag="bank", name="bank")
                 for j in range(BANK // P):
                     c = (BANK // P) * i + j
                     nc.tensor.transpose(bank[:, j * P : (j + 1) * P], words[:, c * P : (c + 1) * P], ident_f32[:])
@@ -156,8 +139,11 @@ def tile_littlebititqspeclinear_pa_kernel(
             half = banks[n // 2][:].bitcast(BF16)[:, (n % 2) * K_PASS : (n % 2 + 1) * K_PASS]
             return half.rearrange("p (u r e) -> p r u e", u=2, e=2)
 
-        def prepare_weight(w):
-            banks = transpose_words(raw_w[w], psum_w, "tw")
+        signed = []
+        scaled_x = []
+
+        def sign_weight(w):
+            banks = transpose_words(raw_w[w])
             signs = stage.tile([P, UNITS, P, PACK], BF16, tag="signs", bufs=3, align_bytes=64)
             for n in range(UNITS):
                 nc.scalar.activation(
@@ -165,140 +151,203 @@ def tile_littlebititqspeclinear_pa_kernel(
                     in_=unit_by_row(banks, n),
                     func=ACT.Sign,
                 )
-            if w < BRANCHES * S_TILES:
-                b, t = w // S_TILES, w % S_TILES
-                codes, scales = v_codes[b][:, t, :], v_scales[b][:, t, :]
-            else:
-                og, b = (w - BRANCHES * S_TILES) // BRANCHES, w % BRANCHES
-                codes, scales = u_codes[b][:, og, :], u_scales[b][:, og, :]
-            nc.vector.quantize_mx(
-                out=codes.bitcast(FP8X4), scales=scales, in_=signs[:].rearrange("p n r t -> p (n r t)")
+            signed.append((w, signs))
+
+        def quantise_weights(keep):
+            while len(signed) > keep:
+                w, signs = signed.pop(0)
+                if w < V_WEIGHTS:
+                    b, t = w // S_TILES, w % S_TILES
+                    codes, scales = v_codes[b][:, t, :], v_scales[b][:, t, :]
+                else:
+                    og, b = (w - V_WEIGHTS) // BRANCHES, w % BRANCHES
+                    codes, scales = u_codes[b][:, og, :], u_scales[b][:, og, :]
+                nc.vector.quantize_mx(
+                    out=codes.bitcast(FP8X4), scales=scales, in_=signs[:].rearrange("p n r t -> p (n r t)")
+                )
+
+        def scale_x(pair, g):
+            words = raw_x[pair][:].bitcast(F32)
+            bank = psum.tile([P, BANK], F32, tag="bank", name="bank")
+            for u in range(2):
+                for i in range(2):
+                    first = i * (IN // 2) + (2 * g + u) * P
+                    nc.tensor.transpose(
+                        bank[:, (2 * u + i) * P : (2 * u + i + 1) * P], words[:, first : first + P], ident_f32[:]
+                    )
+            scaled = stage.tile([P, BRANCHES, PAIR, PACK], BF16, tag="scaled", bufs=4, align_bytes=64)
+            for b in range(BRANCHES):
+                first = (b * PASSES + g) * PACK
+                factors = k_vectors[:, first : first + PACK].rearrange("p (u e) -> p u e", u=2)
+                nc.vector.tensor_tensor(
+                    out=scaled[:, b, :, :].rearrange("p r (u e) -> p r u e", u=2),
+                    in0=bank[:].bitcast(BF16).rearrange("p (u r e) -> p r u e", u=2, e=2),
+                    in1=factors.unsqueeze(1).to_broadcast([P, PAIR, 2, 2]),
+                    op=ALU.mult,
+                )
+            scaled_x.append((pair, g, scaled))
+
+        def quantise_x(keep):
+            while len(scaled_x) > keep:
+                pair, g, scaled = scaled_x.pop(0)
+                h, j = pair // PAIRS, pair % PAIRS
+                for b in range(BRANCHES):
+                    nc.vector.quantize_mx(
+                        out=x_codes[b, h][:, g, j * PAIR : (j + 1) * PAIR].bitcast(FP8X4),
+                        scales=x_scales[b, h][:, g, j * PAIR : (j + 1) * PAIR],
+                        in_=scaled[:, b, :, :].rearrange("p r t -> p (r t)"),
+                    )
+
+        grouped_h = {}
+
+        def first_stage(h, b, i):
+            if i == 0:
+                grouped_h[h, b] = stage.tile([P, BANK, PACK], BF16, tag="grouped", name="grouped", align_bytes=64)
+            rows = slice(i * P, (i + 1) * P)
+            acc = psum.tile([P, S_TILES, P], F32, tag="bank", name="bank")
+            for t in range(S_TILES):
+                for g in range(PASSES):
+                    nc.tensor.matmul_mx(
+                        out=acc[:, t, :],
+                        lhsT=v_codes[b][:, t, g * P : (g + 1) * P].bitcast(FP8X4),
+                        lhsT_scale=v_scales[b][:, t, g * P : (g + 1) * P],
+                        rhs=x_codes[b, h][:, g, rows].bitcast(FP8X4),
+                        rhs_scale=x_scales[b, h][:, g, rows],
+                        start=(g == 0),
+                        stop=(g == PASSES - 1),
+                    )
+            nc.vector.tensor_tensor(
+                out=grouped_h[h, b][:, rows, :],
+                in0=acc[:].rearrange("p t r -> p r t"),
+                in1=v1u2[:, b, :].unsqueeze(1).to_broadcast([P, P, PACK]),
+                op=ALU.mult,
             )
 
-        def prepare_x(pair):
-            h, j = pair // PAIRS, pair % PAIRS
-            words = raw_x[pair][:].bitcast(F32)
-            waiting = []
-            for g in range(PASSES + 1):
-                if g < PASSES:
-                    bank = psum_x.tile([P, BANK], F32, tag="tx")
-                    for u in range(2):
-                        for i in range(2):
-                            first = i * (IN // 2) + (2 * g + u) * P
-                            nc.tensor.transpose(
-                                bank[:, (2 * u + i) * P : (2 * u + i + 1) * P], words[:, first : first + P], ident_f32[:]
-                            )
-                    scaled = stage.tile([P, BRANCHES, PAIR, PACK], BF16, tag="scaled", bufs=4, align_bytes=64)
-                    for b in range(BRANCHES):
-                        first = (b * PASSES + g) * PACK
-                        factors = k_vectors[:, first : first + PACK].rearrange("p (u e) -> p u e", u=2)
-                        nc.vector.tensor_tensor(
-                            out=scaled[:, b, :, :].rearrange("p r (u e) -> p r u e", u=2),
-                            in0=bank[:].bitcast(BF16).rearrange("p (u r e) -> p r u e", u=2, e=2),
-                            in1=factors.unsqueeze(1).to_broadcast([P, PAIR, 2, 2]),
-                            op=ALU.mult,
-                        )
-                for ready_g, ready in waiting:
-                    for b in range(BRANCHES):
-                        nc.vector.quantize_mx(
-                            out=x_codes[b, h][:, ready_g, j * PAIR : (j + 1) * PAIR].bitcast(FP8X4),
-                            scales=x_scales[b, h][:, ready_g, j * PAIR : (j + 1) * PAIR],
-                            in_=ready[:, b, :, :].rearrange("p r t -> p (r t)"),
-                        )
-                waiting = [(g, scaled)] if g < PASSES else []
+        def quantise_h(h, b):
+            nc.vector.quantize_mx(
+                out=h_codes[b, h][:].bitcast(FP8X4),
+                scales=h_scales[b, h][:],
+                in_=grouped_h[h, b][:].rearrange("p r t -> p (r t)"),
+            )
 
-        def first_stage(h):
-            for b in range(BRANCHES):
-                planes = stage.tile([P, S_TILES, BANK], BF16, tag="planes")
-                for t in range(S_TILES):
-                    acc = psum_s.tile([P, BANK], F32, tag="acc_s")
-                    for g in range(PASSES):
-                        nc.tensor.matmul_mx(
-                            out=acc[:],
-                            lhsT=v_codes[b][:, t, g * P : (g + 1) * P].bitcast(FP8X4),
-                            lhsT_scale=v_scales[b][:, t, g * P : (g + 1) * P],
-                            rhs=x_codes[b, h][:, g, :].bitcast(FP8X4),
-                            rhs_scale=x_scales[b, h][:, g, :],
-                            start=(g == 0),
-                            stop=(g == PASSES - 1),
-                        )
-                    nc.scalar.activation(out=planes[:, t, :], in_=acc[:], func=ACT.Copy, scale=v1u2[:, b, t : t + 1])
-                grouped = stage.tile([P, BANK, PACK], BF16, tag="grouped", align_bytes=64)
-                nc.vector.tensor_copy(
-                    out=grouped[:].rearrange("p (c i) t -> p c t i", i=4),
-                    in_=planes[:].rearrange("p t (c i) -> p c t i", i=4),
-                )
-                nc.vector.quantize_mx(
-                    out=h_codes[b, h][:].bitcast(FP8X4),
-                    scales=h_scales[b, h][:],
-                    in_=grouped[:].rearrange("p r t -> p (r t)"),
-                )
+        totals = {}
 
-        def second_stage(h, og):
-            total = stage.tile([P, O_TILES, BANK], F32, tag="total", bufs=3)
+        def product(h, og, b, ol):
+            acc = psum.tile([P, BANK], F32, tag="bank", name="bank")
+            nc.tensor.matmul_mx(
+                out=acc[:],
+                lhsT=u_codes[b][:, og, ol * P : (ol + 1) * P].bitcast(FP8X4),
+                lhsT_scale=u_scales[b][:, og, ol * P : (ol + 1) * P],
+                rhs=h_codes[b, h][:].bitcast(FP8X4),
+                rhs_scale=h_scales[b, h][:],
+                start=True,
+                stop=True,
+            )
+            return acc
 
-            def product(pool, tag, b, ol):
-                acc = pool.tile([P, BANK], F32, tag=tag)
-                nc.tensor.matmul_mx(
-                    out=acc[:],
-                    lhsT=u_codes[b][:, og, ol * P : (ol + 1) * P].bitcast(FP8X4),
-                    lhsT_scale=u_scales[b][:, og, ol * P : (ol + 1) * P],
-                    rhs=h_codes[b, h][:].bitcast(FP8X4),
-                    rhs_scale=h_scales[b, h][:],
-                    start=True,
-                    stop=True,
-                )
-                return acc
+        def main_branch(h, og, ol):
+            if ol == 0:
+                totals[h, og] = stage.tile([P, O_TILES, BANK], F32, tag="total", name="total", bufs=3)
+            ot = og * O_TILES + ol
+            nc.scalar.activation(
+                out=totals[h, og][:, ol, :],
+                in_=product(h, og, 0, ol)[:],
+                func=ACT.Identity,
+                scale=o_vectors[:, 0, ot : ot + 1],
+                bias=o_vectors[:, 2, ot : ot + 1],
+            )
 
-            def main_branch(ol):
-                ot = og * O_TILES + ol
-                nc.scalar.activation(
-                    out=total[:, ol, :],
-                    in_=product(psum_s, "acc_s", 0, ol)[:],
-                    func=ACT.Identity,
-                    scale=o_vectors[:, 0, ot : ot + 1],
-                    bias=o_vectors[:, 2, ot : ot + 1],
-                )
+        def add_residual_branch(h, og, ol):
+            ot = og * O_TILES + ol
+            nc.vector.scalar_tensor_tensor(
+                out=totals[h, og][:, ol, :],
+                in0=product(h, og, 1, ol)[:],
+                scalar=o_vectors[:, 1, ot : ot + 1],
+                in1=totals[h, og][:, ol, :],
+                op0=ALU.mult,
+                op1=ALU.add,
+            )
 
-            def add_residual_branch(ol):
-                ot = og * O_TILES + ol
-                nc.vector.scalar_tensor_tensor(
-                    out=total[:, ol, :],
-                    in0=product(psum_v, "acc_v", 1, ol)[:],
-                    scalar=o_vectors[:, 1, ot : ot + 1],
-                    in1=total[:, ol, :],
-                    op0=ALU.mult,
-                    op1=ALU.add,
-                )
-
-            main_branch(0)
+        def store(h, og, j):
+            bank = psum.tile([P, BANK], F32, tag="bank", name="bank")
             for ol in range(O_TILES):
-                if ol + 1 < O_TILES:
-                    main_branch(ol + 1)
-                add_residual_branch(ol)
-            for j in range(X_TILES):
-                bank = psum_w.tile([P, BANK], F32, tag="tw")
-                for ol in range(O_TILES):
-                    nc.tensor.transpose(
-                        bank[:, ol * P : (ol + 1) * P], total[:, ol, j * P : (j + 1) * P], ident_f32[:]
-                    )
-                result = stage.tile([P, BANK], F32, tag="result", bufs=6)
-                if h == HALVES - 1 and j % 2 == 1:
-                    nc.vector.tensor_copy(out=result[:], in_=bank[:])
-                else:
-                    nc.scalar.copy(out=result[:], in_=bank[:])
-                r0 = h * BANK + j * P
-                nc.sync.dma_start(out=out_rows[r0 : r0 + P, og * BANK : (og + 1) * BANK], in_=result[:])
+                nc.tensor.transpose(
+                    bank[:, ol * P : (ol + 1) * P], totals[h, og][:, ol, j * P : (j + 1) * P], ident_f32[:]
+                )
+            result = stage.tile([P, BANK], F32, tag="result", name="result", bufs=6)
+            if h == HALVES - 1 and j % 2 == 1:
+                nc.vector.tensor_copy(out=result[:], in_=bank[:])
+            else:
+                nc.scalar.copy(out=result[:], in_=bank[:])
+            r0 = h * BANK + j * P
+            nc.sync.dma_start(out=out_rows[r0 : r0 + P, og * BANK : (og + 1) * BANK], in_=result[:])
 
-        for j in range(PAIRS):
-            prepare_x(j)
-            for w in range(WEIGHTS_PER_PAIR * j, WEIGHTS_PER_PAIR * (j + 1)):
-                prepare_weight(w)
-        first_stage(0)
-        for j in range(PAIRS):
-            prepare_x(PAIRS + j)
-            second_stage(0, 2 * j)
-            second_stage(0, 2 * j + 1)
-        first_stage(1)
-        for og in range(O_GROUPS):
-            second_stage(1, og)
+        x_passes = [(pair, g) for pair in range(HALVES * PAIRS) for g in range(PASSES)]
+        h_units = [(h, b, i) for h in range(HALVES) for b in range(BRANCHES) for i in range(X_TILES)]
+
+        def next_first_stage():
+            h, b, i = h_units.pop(0)
+            first_stage(h, b, i)
+            if i == 0 and b > 0:
+                quantise_h(h, b - 1)
+
+        sign_weight(0)
+        word_bank = psum.tile([P, BANK], F32, tag="bank", name="bank")
+        nc.tensor.transpose(word_bank[:, 0:P], word_rows[:].bitcast(F32), ident_f32[:])
+        k_vectors = consts.tile([P, WORD_COLS], BF16)
+        nc.vector.tensor_copy(out=k_vectors[:], in_=word_bank[:].bitcast(BF16)[:, 0:WORD_COLS])
+        V2_COLS = BRANCHES * PASSES * PACK
+        v1_and_u2 = k_vectors[:, V2_COLS:WORD_COLS].rearrange("p (b w t) -> p b w t", b=BRANCHES, w=2)
+        v1u2 = consts.tile([P, BRANCHES, PACK], F32)
+        nc.vector.tensor_tensor(out=v1u2[:], in0=v1_and_u2[:, :, 0, :], in1=v1_and_u2[:, :, 1, :], op=ALU.mult)
+        for w in range(V_WEIGHTS):
+            if w > 0:
+                sign_weight(w)
+            scale_x(*x_passes.pop(0))
+            quantise_x(keep=1)
+            quantise_weights(keep=1)
+        next_u = V_WEIGHTS
+        for n in range(BRANCHES * X_TILES):
+            if n in (0, 1, 3, 4, 6):
+                sign_weight(next_u)
+                next_u += 1
+            if n == 0:
+                quantise_x(keep=0)
+                quantise_weights(keep=1)
+            next_first_stage()
+            quantise_weights(keep=1)
+        out_vec_bank = psum.tile([P, P], BF16, tag="bank", name="bank")
+        nc.tensor.transpose(out_vec_bank[:], out_vec_rows[:], ident_bf16[:])
+        o_vectors = consts.tile([P, 3, OUT_COLS], F32)
+        nc.vector.tensor_copy(
+            out=o_vectors[:].rearrange("p v c -> p (v c)"), in_=out_vec_bank[:, 0 : 3 * OUT_COLS]
+        )
+        quantise_h(0, BRANCHES - 1)
+        last = None
+        for h in range(HALVES):
+            for og in range(O_GROUPS):
+                main_branch(h, og, 0)
+                for ol in range(O_TILES):
+                    step = og * O_TILES + ol
+                    if ol + 1 < O_TILES:
+                        main_branch(h, og, ol + 1)
+                    add_residual_branch(h, og, ol)
+                    if last and ol % 2 == 1:
+                        store(last[0], last[1], ol - 1)
+                        store(last[0], last[1], ol)
+                    if h == 0:
+                        if step % 3 == 0 and next_u < WEIGHTS:
+                            sign_weight(next_u)
+                            next_u += 1
+                        if x_passes:
+                            scale_x(*x_passes.pop(0))
+                            quantise_x(keep=1)
+                        elif h_units:
+                            quantise_x(keep=0)
+                            next_first_stage()
+                        quantise_weights(keep=0 if ol == O_TILES - 1 else 1)
+                last = (h, og)
+            if h == 0:
+                quantise_h(1, BRANCHES - 1)
+        for j in range(X_TILES):
+            store(last[0], last[1], j)

@@ -94,19 +94,26 @@ def tile_littlebititqspeclinear_pa_kernel(
                 nc.sync.dma_start(out=raw[:].rearrange("p (n s) -> p n s", n=O_TILES), in_=weight_views[w])
             return raw
 
-        def load_x(pair):
-            raw = raws_x.tile([P, 2 * IN], BF16, tag="raw_x", name="raw_x%d" % pair)
-            nc.sync.dma_start(out=raw[:].rearrange("p (i k) -> p i k", i=2), in_=x_views[pair])
-            return raw
+        def load_x(pair, first_pass, passes):
+            cols = slice(first_pass * K_PASS, (first_pass + passes) * K_PASS)
+            width = passes * K_PASS
+            if passes == PASSES:
+                raw = raws_x.tile([P, 2 * width], BF16, tag="raw_x", name="raw_x")
+            else:
+                raw = raws_x.tile([P, 2 * width], BF16, tag="raw_x_pass", name="raw_x_pass", bufs=PASSES)
+            nc.sync.dma_start(out=raw[:].rearrange("p (i k) -> p i k", i=2), in_=x_views[pair][:, :, cols])
+            words = raw[:].bitcast(F32).rearrange("p (i w) -> p i w", i=2)
+            for g in range(passes):
+                x_words[pair, first_pass + g] = words[:, :, g * 2 * P : (g + 1) * 2 * P]
 
         ctx.enter_context(tc.manual_schedule())
         raw_w = {}
-        raw_x = {}
-        for pair, before in enumerate((1, 4, 10, 12)):
-            for w in range(len(raw_w), before):
-                raw_w[w] = load_weight(w)
-            raw_x[pair] = load_x(pair)
-        for w in range(len(raw_w), WEIGHTS):
+        x_words = {}
+        for w in range(WEIGHTS):
+            if w < PASSES:
+                load_x(0, w, 1)
+            elif w in (4, 10, 12):
+                load_x({4: 1, 10: 2, 12: 3}[w], 0, PASSES)
             raw_w[w] = load_weight(w)
 
         v_codes = [keep.tile([P, S_TILES, K_PASS], U32, name="v_codes%d" % b, align_bytes=64) for b in range(2)]
@@ -117,38 +124,31 @@ def tile_littlebititqspeclinear_pa_kernel(
         x_scales = {}
         h_codes = {}
         h_scales = {}
+        for pair in range(HALVES * PAIRS):
+            x_codes[pair] = keep.tile([P, PASSES, BRANCHES * PAIR], U32, name="x_codes%d" % pair, align_bytes=64)
+            x_scales[pair] = keep.tile([P, PASSES, BRANCHES * PAIR], U8, name="x_scales%d" % pair, align_bytes=64)
         for b in range(BRANCHES):
             for h in range(HALVES):
-                x_codes[b, h] = keep.tile([P, PASSES, BANK], U32, name="x_codes%d%d" % (b, h), align_bytes=64)
-                x_scales[b, h] = keep.tile([P, PASSES, BANK], U8, name="x_scales%d%d" % (b, h), align_bytes=64)
                 h_codes[b, h] = keep.tile([P, BANK], U32, name="h_codes%d%d" % (b, h), align_bytes=64)
                 h_scales[b, h] = keep.tile([P, BANK], U8, name="h_scales%d%d" % (b, h), align_bytes=64)
-
-        def transpose_words(raw):
-            words = raw[:].bitcast(F32)
-            banks = []
-            for i in range(2):
-                bank = psum.tile([P, BANK], F32, tag="bank", name="bank")
-                for j in range(BANK // P):
-                    c = (BANK // P) * i + j
-                    nc.tensor.transpose(bank[:, j * P : (j + 1) * P], words[:, c * P : (c + 1) * P], ident_f32[:])
-                banks.append(bank)
-            return banks
-
-        def unit_by_row(banks, n):
-            half = banks[n // 2][:].bitcast(BF16)[:, (n % 2) * K_PASS : (n % 2 + 1) * K_PASS]
-            return half.rearrange("p (u r e) -> p r u e", u=2, e=2)
 
         signed = []
         scaled_x = []
 
         def sign_weight(w):
-            banks = transpose_words(raw_w[w])
-            signs = stage.tile([P, UNITS, P, PACK], BF16, tag="signs", bufs=3, align_bytes=64)
-            for n in range(UNITS):
+            words = raw_w[w][:].bitcast(F32)
+            signs = stage.tile([P, UNITS * P, PACK], BF16, tag="signs", bufs=3, align_bytes=64)
+            for i in range(UNITS // 2):
+                bank = psum.tile([P, BANK], F32, tag="bank", name="bank")
+                for u in range(2):
+                    for n in range(2):
+                        first = (2 * (2 * i + n) + u) * P
+                        nc.tensor.transpose(
+                            bank[:, (2 * u + n) * P : (2 * u + n + 1) * P], words[:, first : first + P], ident_f32[:]
+                        )
                 nc.scalar.activation(
-                    out=signs[:, n, :, :].rearrange("p r (u e) -> p r u e", u=2),
-                    in_=unit_by_row(banks, n),
+                    out=signs[:, i * 2 * P : (i + 1) * 2 * P, :].rearrange("p q (u e) -> p q u e", u=2),
+                    in_=bank[:].bitcast(BF16).rearrange("p (u q e) -> p q u e", u=2, e=2),
                     func=ACT.Sign,
                 )
             signed.append((w, signs))
@@ -163,17 +163,16 @@ def tile_littlebititqspeclinear_pa_kernel(
                     og, b = (w - V_WEIGHTS) // BRANCHES, w % BRANCHES
                     codes, scales = u_codes[b][:, og, :], u_scales[b][:, og, :]
                 nc.vector.quantize_mx(
-                    out=codes.bitcast(FP8X4), scales=scales, in_=signs[:].rearrange("p n r t -> p (n r t)")
+                    out=codes.bitcast(FP8X4), scales=scales, in_=signs[:].rearrange("p q t -> p (q t)")
                 )
 
         def scale_x(pair, g):
-            words = raw_x[pair][:].bitcast(F32)
+            words = x_words[pair, g]
             bank = psum.tile([P, BANK], F32, tag="bank", name="bank")
             for u in range(2):
                 for i in range(2):
-                    first = i * (IN // 2) + (2 * g + u) * P
                     nc.tensor.transpose(
-                        bank[:, (2 * u + i) * P : (2 * u + i + 1) * P], words[:, first : first + P], ident_f32[:]
+                        bank[:, (2 * u + i) * P : (2 * u + i + 1) * P], words[:, i, u * P : (u + 1) * P], ident_f32[:]
                     )
             scaled = stage.tile([P, BRANCHES, PAIR, PACK], BF16, tag="scaled", bufs=4, align_bytes=64)
             for b in range(BRANCHES):
@@ -190,13 +189,11 @@ def tile_littlebititqspeclinear_pa_kernel(
         def quantise_x(keep):
             while len(scaled_x) > keep:
                 pair, g, scaled = scaled_x.pop(0)
-                h, j = pair // PAIRS, pair % PAIRS
-                for b in range(BRANCHES):
-                    nc.vector.quantize_mx(
-                        out=x_codes[b, h][:, g, j * PAIR : (j + 1) * PAIR].bitcast(FP8X4),
-                        scales=x_scales[b, h][:, g, j * PAIR : (j + 1) * PAIR],
-                        in_=scaled[:, b, :, :].rearrange("p r t -> p (r t)"),
-                    )
+                nc.vector.quantize_mx(
+                    out=x_codes[pair][:, g, :].bitcast(FP8X4),
+                    scales=x_scales[pair][:, g, :],
+                    in_=scaled[:].rearrange("p b r t -> p (b r t)"),
+                )
 
         grouped_h = {}
 
@@ -204,6 +201,9 @@ def tile_littlebititqspeclinear_pa_kernel(
             if i == 0:
                 grouped_h[h, b] = stage.tile([P, BANK, PACK], BF16, tag="grouped", name="grouped", align_bytes=64)
             rows = slice(i * P, (i + 1) * P)
+            pair = (h * BANK + i * P) // PAIR
+            first = b * PAIR + (i * P) % PAIR
+            x_cols = slice(first, first + P)
             acc = psum.tile([P, S_TILES, P], F32, tag="bank", name="bank")
             for t in range(S_TILES):
                 for g in range(PASSES):
@@ -211,8 +211,8 @@ def tile_littlebititqspeclinear_pa_kernel(
                         out=acc[:, t, :],
                         lhsT=v_codes[b][:, t, g * P : (g + 1) * P].bitcast(FP8X4),
                         lhsT_scale=v_scales[b][:, t, g * P : (g + 1) * P],
-                        rhs=x_codes[b, h][:, g, rows].bitcast(FP8X4),
-                        rhs_scale=x_scales[b, h][:, g, rows],
+                        rhs=x_codes[pair][:, g, x_cols].bitcast(FP8X4),
+                        rhs_scale=x_scales[pair][:, g, x_cols],
                         start=(g == 0),
                         stop=(g == PASSES - 1),
                     )
@@ -291,7 +291,6 @@ def tile_littlebititqspeclinear_pa_kernel(
             if i == 0 and b > 0:
                 quantise_h(h, b - 1)
 
-        sign_weight(0)
         word_bank = psum.tile([P, BANK], F32, tag="bank", name="bank")
         nc.tensor.transpose(word_bank[:, 0:P], word_rows[:].bitcast(F32), ident_f32[:])
         k_vectors = consts.tile([P, WORD_COLS], BF16)
@@ -301,9 +300,8 @@ def tile_littlebititqspeclinear_pa_kernel(
         v1u2 = consts.tile([P, BRANCHES, PACK], F32)
         nc.vector.tensor_tensor(out=v1u2[:], in0=v1_and_u2[:, :, 0, :], in1=v1_and_u2[:, :, 1, :], op=ALU.mult)
         for w in range(V_WEIGHTS):
-            if w > 0:
-                sign_weight(w)
             scale_x(*x_passes.pop(0))
+            sign_weight(w)
             quantise_x(keep=1)
             quantise_weights(keep=1)
         next_u = V_WEIGHTS

@@ -97,10 +97,8 @@ def tile_littlebititqspeclinear_pa_kernel(
         def load_x(pair, first_pass, passes):
             cols = slice(first_pass * K_PASS, (first_pass + passes) * K_PASS)
             width = passes * K_PASS
-            if passes == PASSES:
-                raw = raws_x.tile([P, 2 * width], BF16, tag="raw_x", name="raw_x")
-            else:
-                raw = raws_x.tile([P, 2 * width], BF16, tag="raw_x_pass", name="raw_x_pass", bufs=PASSES)
+            tag = "raw_x%d" % passes
+            raw = raws_x.tile([P, 2 * width], BF16, tag=tag, name=tag, bufs=max(2, PASSES // passes))
             nc.sync.dma_start(out=raw[:].rearrange("p (i k) -> p i k", i=2), in_=x_views[pair][:, :, cols])
             words = raw[:].bitcast(F32).rearrange("p (i w) -> p i w", i=2)
             for g in range(passes):
@@ -112,8 +110,10 @@ def tile_littlebititqspeclinear_pa_kernel(
         for w in range(WEIGHTS):
             if w < PASSES:
                 load_x(0, w, 1)
-            elif w in (4, 10, 12):
-                load_x({4: 1, 10: 2, 12: 3}[w], 0, PASSES)
+            elif w in (4, 6):
+                load_x(1, w - 4, 2)
+            elif w in (10, 12):
+                load_x({10: 2, 12: 3}[w], 0, PASSES)
             raw_w[w] = load_weight(w)
 
         v_codes = [keep.tile([P, S_TILES, K_PASS], U32, name="v_codes%d" % b, align_bytes=64) for b in range(2)]
@@ -285,11 +285,18 @@ def tile_littlebititqspeclinear_pa_kernel(
         x_passes = [(pair, g) for pair in range(HALVES * PAIRS) for g in range(PASSES)]
         h_units = [(h, b, i) for h in range(HALVES) for b in range(BRANCHES) for i in range(X_TILES)]
 
+        full_h = []
+
         def next_first_stage():
             h, b, i = h_units.pop(0)
             first_stage(h, b, i)
-            if i == 0 and b > 0:
-                quantise_h(h, b - 1)
+            quantise_full_h()
+            if i == X_TILES - 1:
+                full_h.append((h, b))
+
+        def quantise_full_h():
+            while full_h:
+                quantise_h(*full_h.pop(0))
 
         word_bank = psum.tile([P, BANK], F32, tag="bank", name="bank")
         nc.tensor.transpose(word_bank[:, 0:P], word_rows[:].bitcast(F32), ident_f32[:])
@@ -304,23 +311,26 @@ def tile_littlebititqspeclinear_pa_kernel(
             sign_weight(w)
             quantise_x(keep=1)
             quantise_weights(keep=1)
-        next_u = V_WEIGHTS
-        for n in range(BRANCHES * X_TILES):
-            if n in (0, 1, 3, 4, 6):
-                sign_weight(next_u)
-                next_u += 1
-            if n == 0:
-                quantise_x(keep=0)
-                quantise_weights(keep=1)
-            next_first_stage()
-            quantise_weights(keep=1)
         out_vec_bank = psum.tile([P, P], BF16, tag="bank", name="bank")
         nc.tensor.transpose(out_vec_bank[:], out_vec_rows[:], ident_bf16[:])
         o_vectors = consts.tile([P, 3, OUT_COLS], F32)
         nc.vector.tensor_copy(
             out=o_vectors[:].rearrange("p v c -> p (v c)"), in_=out_vec_bank[:, 0 : 3 * OUT_COLS]
         )
-        quantise_h(0, BRANCHES - 1)
+        next_u = V_WEIGHTS
+        for n in range(BRANCHES * X_TILES):
+            if n % 2 == 0:
+                sign_weight(next_u)
+                next_u += 1
+            if n == 0:
+                quantise_x(keep=0)
+                quantise_weights(keep=1)
+            next_first_stage()
+            if n in (2, 5):
+                scale_x(*x_passes.pop(0))
+                quantise_x(keep=1)
+            quantise_weights(keep=1)
+        quantise_full_h()
         last = None
         for h in range(HALVES):
             for og in range(O_GROUPS):
@@ -330,22 +340,22 @@ def tile_littlebititqspeclinear_pa_kernel(
                     if ol + 1 < O_TILES:
                         main_branch(h, og, ol + 1)
                     add_residual_branch(h, og, ol)
+                    quantise_full_h()
                     if last and ol % 2 == 1:
                         store(last[0], last[1], ol - 1)
                         store(last[0], last[1], ol)
                     if h == 0:
-                        if step % 3 == 0 and next_u < WEIGHTS:
+                        if step % 2 == 1 and next_u < WEIGHTS:
                             sign_weight(next_u)
                             next_u += 1
-                        if x_passes:
+                        if step % 3 < 2 and x_passes:
                             scale_x(*x_passes.pop(0))
                             quantise_x(keep=1)
-                        elif h_units:
+                        if step >= 8:
                             quantise_x(keep=0)
-                            next_first_stage()
+                            for unit in range(min(1 + step % 2, len(h_units))):
+                                next_first_stage()
                         quantise_weights(keep=0 if ol == O_TILES - 1 else 1)
                 last = (h, og)
-            if h == 0:
-                quantise_h(1, BRANCHES - 1)
         for j in range(X_TILES):
             store(last[0], last[1], j)

@@ -283,7 +283,13 @@ def tile_littlebititqspeclinear_pa_kernel(
             nc.sync.dma_start(out=out_rows[r0 : r0 + P, og * BANK : (og + 1) * BANK], in_=result[:])
 
         x_passes = [(pair, g) for pair in range(HALVES * PAIRS) for g in range(PASSES)]
-        h_units = [(h, b, i) for h in range(HALVES) for b in range(BRANCHES) for i in range(X_TILES)]
+        h_units = [
+            (h, b, 2 * pair + i)
+            for h in range(HALVES)
+            for pair in range(PAIRS)
+            for b in range(BRANCHES)
+            for i in range(2)
+        ]
 
         full_h = []
 
@@ -319,6 +325,9 @@ def tile_littlebititqspeclinear_pa_kernel(
         )
         next_u = V_WEIGHTS
         for n in range(BRANCHES * X_TILES):
+            if n % 4 == 2:
+                scale_x(*x_passes.pop(0))
+                quantise_x(keep=1)
             if n % 2 == 0:
                 sign_weight(next_u)
                 next_u += 1
@@ -326,9 +335,6 @@ def tile_littlebititqspeclinear_pa_kernel(
                 quantise_x(keep=0)
                 quantise_weights(keep=1)
             next_first_stage()
-            if n in (2, 5):
-                scale_x(*x_passes.pop(0))
-                quantise_x(keep=1)
             quantise_weights(keep=1)
         quantise_full_h()
         last = None
@@ -348,12 +354,13 @@ def tile_littlebititqspeclinear_pa_kernel(
                         if step % 2 == 1 and next_u < WEIGHTS:
                             sign_weight(next_u)
                             next_u += 1
-                        if step % 3 < 2 and x_passes:
+                        if (step == 0 or step % 2 == 1) and x_passes:
                             scale_x(*x_passes.pop(0))
                             quantise_x(keep=1)
-                        if step >= 8:
+                        if not x_passes:
                             quantise_x(keep=0)
-                            for unit in range(min(1 + step % 2, len(h_units))):
+                        if step > 5 and step % 2 == 1:
+                            for unit in range(min(2, len(h_units))):
                                 next_first_stage()
                         quantise_weights(keep=0 if ol == O_TILES - 1 else 1)
                 last = (h, og)

@@ -68,12 +68,10 @@ def tile_littlebititqspeclinear_pa_kernel(
         out_vec_rows = consts.tile([P, P], BF16)
         nc.vector.memset(out_vec_rows[:], 0.0)
         OUT_COLS = OUT // P
-        nc.gpsimd.dma_start(out=out_vec_rows[0:OUT_COLS, :], in_=u1.rearrange("o (c w) -> (o c) w", w=P))
-        nc.gpsimd.dma_start(
-            out=out_vec_rows[OUT_COLS : 2 * OUT_COLS, :], in_=u1_R.rearrange("o (c w) -> (o c) w", w=P)
-        )
-        nc.gpsimd.dma_start(
-            out=out_vec_rows[2 * OUT_COLS : 3 * OUT_COLS, :], in_=bias.rearrange("(c w) -> c w", w=P)
+        out_vectors = (
+            u1.rearrange("o (c w) -> (o c) w", w=P),
+            u1_R.rearrange("o (c w) -> (o c) w", w=P),
+            bias.rearrange("(c w) -> c w", w=P),
         )
 
         weight_views = []
@@ -115,6 +113,9 @@ def tile_littlebititqspeclinear_pa_kernel(
             elif w in (10, 12):
                 load_x({10: 2, 12: 3}[w], 0, PASSES)
             raw_w[w] = load_weight(w)
+            if w == PASSES:
+                for n, rows in enumerate(out_vectors):
+                    nc.sync.dma_start(out=out_vec_rows[n * OUT_COLS : (n + 1) * OUT_COLS, :], in_=rows)
 
         v_codes = [keep.tile([P, S_TILES, K_PASS], U32, name="v_codes%d" % b, align_bytes=64) for b in range(2)]
         v_scales = [keep.tile([P, S_TILES, K_PASS], U8, name="v_scales%d" % b, align_bytes=64) for b in range(2)]

@@ -31,6 +31,7 @@ V_WEIGHTS = BRANCHES * S_TILES
 WEIGHTS = V_WEIGHTS + BRANCHES * O_GROUPS
 RAW_W_SLOTS = 8
 RAW_X_SLOTS = 2
+DIRECT_GROUP = 0
 BANKS = 8
 
 FLOPS = 2 * BRANCHES * (ROWS * IN * SPLIT + ROWS * SPLIT * OUT)
@@ -102,6 +103,8 @@ def tile_littlebititqspeclinear_pa_kernel(
             for g in range(passes):
                 x_words[pair, first_pass + g] = words[:, :, g * 2 * P : (g + 1) * 2 * P]
 
+        direct_vectors = consts.tile([P, 3, BANK], BF16)
+
         ctx.enter_context(tc.manual_schedule())
         raw_w = {}
         x_words = {}
@@ -116,6 +119,9 @@ def tile_littlebititqspeclinear_pa_kernel(
             if w == PASSES:
                 for n, rows in enumerate(out_vectors):
                     nc.sync.dma_start(out=out_vec_rows[n * OUT_COLS : (n + 1) * OUT_COLS, :], in_=rows)
+        direct_cols = slice(DIRECT_GROUP * BANK, (DIRECT_GROUP + 1) * BANK)
+        for n, vector in enumerate((u1[0, direct_cols], u1_R[0, direct_cols], bias[direct_cols])):
+            nc.sync.dma_start(out=direct_vectors[:, n, :], in_=vector.partition_broadcast(P))
 
         v_codes = [keep.tile([P, S_TILES, K_PASS], U32, name="v_codes%d" % b, align_bytes=64) for b in range(2)]
         v_scales = [keep.tile([P, S_TILES, K_PASS], U8, name="v_scales%d" % b, align_bytes=64) for b in range(2)]
@@ -258,6 +264,32 @@ def tile_littlebititqspeclinear_pa_kernel(
                 bias=o_vectors[:, 2, ot : ot + 1],
             )
 
+        direct_results = []
+
+        def direct(h, og, j):
+            rows = slice(j * P, (j + 1) * P)
+            terms = raws_w.tile([P, IN], BF16, tag="raw_w", name="terms")[:].bitcast(F32)
+            terms = terms.rearrange("p (b o) -> p b o", b=BRANCHES)
+            for b in range(BRANCHES):
+                acc = psum.tile([P, BANK], F32, tag="bank", name="bank")
+                nc.tensor.matmul_mx(
+                    out=acc[:],
+                    lhsT=h_codes[b, h][:, rows].bitcast(FP8X4),
+                    lhsT_scale=h_scales[b, h][:, rows],
+                    rhs=u_codes[b][:, og, :].bitcast(FP8X4),
+                    rhs_scale=u_scales[b][:, og, :],
+                    start=True,
+                    stop=True,
+                )
+                nc.vector.tensor_tensor(out=terms[:, b, :], in0=acc[:], in1=direct_vectors[:, b, :], op=ALU.mult)
+            nc.gpsimd.tensor_tensor(out=terms[:, 0, :], in0=terms[:, 0, :], in1=terms[:, 1, :], op=ALU.add)
+            nc.gpsimd.tensor_tensor(out=terms[:, 0, :], in0=terms[:, 0, :], in1=direct_vectors[:, BRANCHES, :], op=ALU.add)
+            direct_results.append((h, og, j, terms))
+
+        def store_direct(h, og, j, terms):
+            r0 = h * BANK + j * P
+            nc.sync.dma_start(out=out_rows[r0 : r0 + P, og * BANK : (og + 1) * BANK], in_=terms[:, 0, :])
+
         def add_residual_branch(h, og, ol):
             ot = og * O_TILES + ol
             nc.vector.scalar_tensor_tensor(
@@ -275,8 +307,8 @@ def tile_littlebititqspeclinear_pa_kernel(
                 nc.tensor.transpose(
                     bank[:, ol * P : (ol + 1) * P], totals[h, og][:, ol, j * P : (j + 1) * P], ident_f32[:]
                 )
-            result = stage.tile([P, BANK], F32, tag="result", name="result", bufs=6)
-            if h == HALVES - 1 and j % 2 == 1:
+            result = stage.tile([P, BANK], F32, tag="result", name="result", bufs=8)
+            if h == HALVES - 1 and og >= O_GROUPS - 2 and j % 2 == 1:
                 nc.vector.tensor_copy(out=result[:], in_=bank[:])
             else:
                 nc.scalar.copy(out=result[:], in_=bank[:])
@@ -338,32 +370,37 @@ def tile_littlebititqspeclinear_pa_kernel(
             next_first_stage()
             quantise_weights(keep=1)
         quantise_full_h()
-        last = None
-        for h in range(HALVES):
-            for og in range(O_GROUPS):
-                main_branch(h, og, 0)
-                for ol in range(O_TILES):
-                    step = og * O_TILES + ol
-                    if ol + 1 < O_TILES:
-                        main_branch(h, og, ol + 1)
-                    add_residual_branch(h, og, ol)
-                    quantise_full_h()
-                    if last and ol % 2 == 1:
-                        store(last[0], last[1], ol - 1)
-                        store(last[0], last[1], ol)
-                    if h == 0:
-                        if step % 2 == 1 and next_u < WEIGHTS:
-                            sign_weight(next_u)
-                            next_u += 1
-                        if (step == 0 or step % 2 == 1) and x_passes:
-                            scale_x(*x_passes.pop(0))
-                            quantise_x(keep=1)
-                        if not x_passes:
-                            quantise_x(keep=0)
-                        if step > 5 and step % 2 == 1:
-                            for unit in range(min(2, len(h_units))):
-                                next_first_stage()
-                        quantise_weights(keep=0 if ol == O_TILES - 1 else 1)
-                last = (h, og)
-        for j in range(X_TILES):
-            store(last[0], last[1], j)
+        steps = [(h, og, ol) for h in range(HALVES) for og in range(O_GROUPS) for ol in range(O_TILES)]
+        mains = [(h, og, ol) for h, og, ol in steps if (h, og) != (HALVES - 1, DIRECT_GROUP)]
+        main_count = len(mains)
+        waiting = []
+        for step, (h, og, ol) in enumerate(steps):
+            while main_count - len(mains) < min(step + 2, main_count):
+                main_branch(*mains.pop(0))
+            if (h, og) == (HALVES - 1, DIRECT_GROUP):
+                direct(h, og, ol)
+            else:
+                add_residual_branch(h, og, ol)
+                if direct_results and step % 3 == 2:
+                    store_direct(*direct_results.pop(0))
+            quantise_full_h()
+            if ol % 2 == 1:
+                for tile in range(min(2, len(waiting))):
+                    store(*waiting.pop(0))
+            if h == 0:
+                if step % 2 == 1 and next_u < WEIGHTS:
+                    sign_weight(next_u)
+                    next_u += 1
+                if (step == 0 or step % 2 == 1) and x_passes:
+                    scale_x(*x_passes.pop(0))
+                    quantise_x(keep=1)
+                if not x_passes:
+                    quantise_x(keep=0)
+                if step > 5 and step % 2 == 1:
+                    for unit in range(min(2, len(h_units))):
+                        next_first_stage()
+                quantise_weights(keep=0 if ol == O_TILES - 1 else 1)
+            if ol == O_TILES - 1 and (h, og) != (HALVES - 1, DIRECT_GROUP):
+                waiting += [(h, og, j) for j in range(X_TILES)]
+        for tile in waiting:
+            store(*tile)

@@ -97,7 +97,7 @@ def tile_littlebititqspeclinear_pa_kernel(
             cols = slice(first_pass * K_PASS, (first_pass + passes) * K_PASS)
             width = passes * K_PASS
             tag = "raw_x%d" % passes
-            raw = raws_x.tile([P, 2 * width], BF16, tag=tag, name=tag, bufs=max(2, PASSES // passes))
+            raw = raws_x.tile([P, 2 * width], BF16, tag=tag, name=tag, bufs=2 * (PASSES // passes))
             nc.sync.dma_start(out=raw[:].rearrange("p (i k) -> p i k", i=2), in_=x_views[pair][:, :, cols])
             words = raw[:].bitcast(F32).rearrange("p (i w) -> p i w", i=2)
             for g in range(passes):
@@ -109,10 +109,8 @@ def tile_littlebititqspeclinear_pa_kernel(
         raw_w = {}
         x_words = {}
         for w in range(WEIGHTS):
-            if w < PASSES:
-                load_x(0, w, 1)
-            elif w in (4, 6):
-                load_x(1, w - 4, 2)
+            if w < V_WEIGHTS and w % 2 == 0:
+                load_x(w // PASSES, w % PASSES, 2)
             elif w in (10, 12):
                 load_x({10: 2, 12: 3}[w], 0, PASSES)
             raw_w[w] = load_weight(w)

@@ -54,8 +54,6 @@ def tile_littlebititqspeclinear_pa_kernel(
 
         ident_f32 = consts.tile([P, P], F32)
         make_identity(nc, ident_f32[:])
-        ident_bf16 = consts.tile([P, P], BF16)
-        make_identity(nc, ident_bf16[:])
 
         word_rows = consts.tile([P, 2 * P], BF16)
         nc.vector.memset(word_rows[:], 0.0)
@@ -66,13 +64,12 @@ def tile_littlebititqspeclinear_pa_kernel(
             first_row += rows.shape[0]
         WORD_COLS = 2 * first_row
 
-        out_vec_rows = consts.tile([P, P], BF16)
+        out_vec_rows = consts.tile([P, BANK], BF16)
         nc.vector.memset(out_vec_rows[:], 0.0)
-        OUT_COLS = OUT // P
         out_vectors = (
-            u1.rearrange("o (c w) -> (o c) w", w=P),
-            u1_R.rearrange("o (c w) -> (o c) w", w=P),
-            bias.rearrange("(c w) -> c w", w=P),
+            u1.rearrange("o (g w) -> (o g) w", w=BANK),
+            u1_R.rearrange("o (g w) -> (o g) w", w=BANK),
+            bias.rearrange("(g w) -> g w", w=BANK),
         )
 
         weight_views = []
@@ -82,15 +79,12 @@ def tile_littlebititqspeclinear_pa_kernel(
                 weight_views.append(by_code[t // 2, t % 2])
         for og in range(O_GROUPS):
             for matrix in (U, U_R):
-                weight_views.append(matrix.rearrange("(g n p) s -> g p n s", n=O_TILES, p=P)[og])
+                weight_views.append(matrix.rearrange("(g p n) s -> g p (n s)", n=O_TILES, p=P)[og])
         x_views = x_rows.rearrange("(n i p) k -> n p i k", i=2, p=P)
 
         def load_weight(w):
             raw = raws_w.tile([P, IN], BF16, tag="raw_w", name="raw_w%d" % w)
-            if w < BRANCHES * S_TILES:
-                nc.sync.dma_start(out=raw[:], in_=weight_views[w])
-            else:
-                nc.sync.dma_start(out=raw[:].rearrange("p (n s) -> p n s", n=O_TILES), in_=weight_views[w])
+            nc.sync.dma_start(out=raw[:], in_=weight_views[w])
             return raw
 
         def load_x(pair, first_pass, passes):
@@ -116,7 +110,7 @@ def tile_littlebititqspeclinear_pa_kernel(
             raw_w[w] = load_weight(w)
             if w == PASSES:
                 for n, rows in enumerate(out_vectors):
-                    nc.sync.dma_start(out=out_vec_rows[n * OUT_COLS : (n + 1) * OUT_COLS, :], in_=rows)
+                    nc.sync.dma_start(out=out_vec_rows[n * O_GROUPS : (n + 1) * O_GROUPS, :], in_=rows)
         direct_cols = slice(DIRECT_GROUP * BANK, (DIRECT_GROUP + 1) * BANK)
         for n, vector in enumerate((u1[0, direct_cols], u1_R[0, direct_cols], bias[direct_cols])):
             nc.sync.dma_start(out=direct_vectors[:, n, :], in_=vector.partition_broadcast(P))
@@ -253,13 +247,12 @@ def tile_littlebititqspeclinear_pa_kernel(
         def main_branch(h, og, ol):
             if ol == 0:
                 totals[h, og] = stage.tile([P, O_TILES, BANK], F32, tag="total", name="total", bufs=3)
-            ot = og * O_TILES + ol
             nc.scalar.activation(
                 out=totals[h, og][:, ol, :],
                 in_=product(h, og, 0, ol)[:],
                 func=ACT.Identity,
-                scale=o_vectors[:, 0, ot : ot + 1],
-                bias=o_vectors[:, 2, ot : ot + 1],
+                scale=o_vectors[:, og, ol : ol + 1],
+                bias=o_vectors[:, 2 * O_GROUPS + og, ol : ol + 1],
             )
 
         direct_results = []
@@ -279,7 +272,12 @@ def tile_littlebititqspeclinear_pa_kernel(
                     start=True,
                     stop=True,
                 )
-                nc.vector.tensor_tensor(out=terms[:, b, :], in0=acc[:], in1=direct_vectors[:, b, :], op=ALU.mult)
+                nc.vector.tensor_tensor(
+                    out=terms[:, b, :].rearrange("p (q n) -> p q n", n=O_TILES),
+                    in0=acc[:].rearrange("p (n q) -> p q n", n=O_TILES),
+                    in1=direct_vectors[:, b, :].rearrange("p (q n) -> p q n", n=O_TILES),
+                    op=ALU.mult,
+                )
             nc.gpsimd.tensor_tensor(out=terms[:, 0, :], in0=terms[:, 0, :], in1=terms[:, 1, :], op=ALU.add)
             nc.gpsimd.tensor_tensor(out=terms[:, 0, :], in0=terms[:, 0, :], in1=direct_vectors[:, BRANCHES, :], op=ALU.add)
             direct_results.append((h, og, j, terms))
@@ -289,11 +287,10 @@ def tile_littlebititqspeclinear_pa_kernel(
             nc.sync.dma_start(out=out_rows[r0 : r0 + P, og * BANK : (og + 1) * BANK], in_=terms[:, 0, :])
 
         def add_residual_branch(h, og, ol):
-            ot = og * O_TILES + ol
             nc.vector.scalar_tensor_tensor(
                 out=totals[h, og][:, ol, :],
                 in0=product(h, og, 1, ol)[:],
-                scalar=o_vectors[:, 1, ot : ot + 1],
+                scalar=o_vectors[:, O_GROUPS + og, ol : ol + 1],
                 in1=totals[h, og][:, ol, :],
                 op0=ALU.mult,
                 op1=ALU.add,
@@ -306,10 +303,12 @@ def tile_littlebititqspeclinear_pa_kernel(
                     bank[:, ol * P : (ol + 1) * P], totals[h, og][:, ol, j * P : (j + 1) * P], ident_f32[:]
                 )
             result = stage.tile([P, BANK], F32, tag="result", name="result", bufs=8)
+            by_tile = bank[:].rearrange("p (n q) -> p q n", n=O_TILES)
+            in_order = result[:].rearrange("p (q n) -> p q n", n=O_TILES)
             if h == HALVES - 1 and og >= O_GROUPS - 2 and j % 2 == 1:
-                nc.vector.tensor_copy(out=result[:], in_=bank[:])
+                nc.vector.tensor_copy(out=in_order, in_=by_tile)
             else:
-                nc.scalar.copy(out=result[:], in_=bank[:])
+                nc.scalar.copy(out=in_order, in_=by_tile)
             r0 = h * BANK + j * P
             nc.sync.dma_start(out=out_rows[r0 : r0 + P, og * BANK : (og + 1) * BANK], in_=result[:])
 
@@ -348,11 +347,13 @@ def tile_littlebititqspeclinear_pa_kernel(
             sign_weight(w)
             quantise_x(keep=1)
             quantise_weights(keep=1)
-        out_vec_bank = psum.tile([P, P], BF16, tag="bank", name="bank")
-        nc.tensor.transpose(out_vec_bank[:], out_vec_rows[:], ident_bf16[:])
-        o_vectors = consts.tile([P, 3, OUT_COLS], F32)
+        out_vec_bank = psum.tile([P, 2, P], F32, tag="bank", name="bank")
+        for u in range(2):
+            nc.tensor.transpose(out_vec_bank[:, u, :], out_vec_rows[:].bitcast(F32)[:, u::2], ident_f32[:])
+        o_vectors = consts.tile([P, 3 * O_GROUPS, O_TILES], F32)
         nc.vector.tensor_copy(
-            out=o_vectors[:].rearrange("p v c -> p (v c)"), in_=out_vec_bank[:, 0 : 3 * OUT_COLS]
+            out=o_vectors[:].rearrange("p r (u e) -> p u r e", u=2),
+            in_=out_vec_bank[:].bitcast(BF16).rearrange("p u (r e) -> p u r e", e=2)[:, :, 0 : 3 * O_GROUPS, :],
         )
         next_u = V_WEIGHTS
         for n in range(BRANCHES * X_TILES):

from contextlib import ExitStack

import concourse.mybir as mybir
from concourse.masks import make_identity

F32 = mybir.dt.float32
BF16 = mybir.dt.bfloat16
U32 = mybir.dt.uint32
U8 = mybir.dt.uint8
FP8X4 = mybir.dt.float8_e4m3fn_x4
ACT = mybir.ActivationFunctionType
ALU = mybir.AluOpType

P = 128
PACK = 4
K_PASS = P * PACK
BANK = 512

ROWS, IN, SPLIT, OUT = 1024, 2048, 512, 2048
BRANCHES = 2
PASSES = IN // K_PASS
UNITS = 4
HALVES = ROWS // BANK
X_TILES = BANK // P
PAIR = 2 * P
PAIRS = BANK // PAIR
S_TILES = SPLIT // P
O_GROUPS = OUT // BANK
O_TILES = BANK // P
V_WEIGHTS = BRANCHES * S_TILES
WEIGHTS = V_WEIGHTS + BRANCHES * O_GROUPS
RAW_W_SLOTS = 8
RAW_X_SLOTS = 2
DIRECT_GROUP = 0
BANKS = 8

FLOPS = 2 * BRANCHES * (ROWS * IN * SPLIT + ROWS * SPLIT * OUT)


def tile_littlebititqspeclinear_pa_kernel(
    tc, x, V, U, v2, v1, u2, u1, V_R, U_R, v2_R, v1_R, u2_R, u1_R, bias, out
):
    nc = tc.nc
    x_rows = x.flatten_outer_dims()
    out_rows = out.flatten_outer_dims()

    with ExitStack() as ctx:
        consts = ctx.enter_context(tc.tile_pool(name="consts", bufs=1))
        keep = ctx.enter_context(tc.tile_pool(name="keep", bufs=1))
        raws_w = ctx.enter_context(tc.tile_pool(name="raws_w", bufs=RAW_W_SLOTS))
        raws_x = ctx.enter_context(tc.tile_pool(name="raws_x", bufs=RAW_X_SLOTS))
        stage = ctx.enter_context(tc.tile_pool(name="stage", bufs=2))
        psum = ctx.enter_context(tc.psum_pool(name="psum", bufs=BANKS))

        ident_f32 = consts.tile([P, P], F32)
        make_identity(nc, ident_f32[:])

        word_rows = consts.tile([P, 2 * P], BF16)
        nc.vector.memset(word_rows[:], 0.0)
        first_row = 0
        for vector in (v2, v2_R, v1, u2, v1_R, u2_R):
            rows = vector.rearrange("o (c w) -> (o c) w", w=2 * P)
            nc.sync.dma_start(out=word_rows[first_row : first_row + rows.shape[0], :], in_=rows)
            first_row += rows.shape[0]
        WORD_COLS = 2 * first_row

        out_vec_rows = consts.tile([P, BANK], BF16)
        nc.vector.memset(out_vec_rows[:], 0.0)
        out_vectors = (
            u1.rearrange("o (g w) -> (o g) w", w=BANK),
            u1_R.rearrange("o (g w) -> (o g) w", w=BANK),
            bias.rearrange("(g w) -> g w", w=BANK),
        )

        weight_views = []
        for matrix in (V, V_R):
            by_code = matrix.rearrange("(u p e) k -> u e p k", u=2, e=2)
            for t in range(S_TILES):
                weight_views.append(by_code[t // 2, t % 2])
        for og in range(O_GROUPS):
            for matrix in (U, U_R):
                weight_views.append(matrix.rearrange("(g p n) s -> g p (n s)", n=O_TILES, p=P)[og])
        x_views = x_rows.rearrange("(n i p) k -> n p i k", i=2, p=P)

        def load_weight(w):
            raw = raws_w.tile([P, IN], BF16, tag="raw_w", name="raw_w%d" % w)
            nc.sync.dma_start(out=raw[:], in_=weight_views[w])
            return raw

        def load_x(pair, first_pass, passes):
            cols = slice(first_pass * K_PASS, (first_pass + passes) * K_PASS)
            width = passes * K_PASS
            tag = "raw_x%d" % passes
            raw = raws_x.tile([P, 2 * width], BF16, tag=tag, name=tag, bufs=2 * (PASSES // passes))
            nc.sync.dma_start(out=raw[:].rearrange("p (i k) -> p i k", i=2), in_=x_views[pair][:, :, cols])
            words = raw[:].bitcast(F32).rearrange("p (i w) -> p i w", i=2)
            for g in range(passes):
                x_words[pair, first_pass + g] = words[:, :, g * 2 * P : (g + 1) * 2 * P]

        direct_vectors = consts.tile([P, 3, BANK], BF16)

        ctx.enter_context(tc.manual_schedule())
        raw_w = {}
        x_words = {}
        for w in range(WEIGHTS):
            if w < V_WEIGHTS and w % 2 == 0:
                load_x(w // PASSES, w % PASSES, 2)
            elif w in (10, 12):
                load_x({10: 2, 12: 3}[w], 0, PASSES)
            raw_w[w] = load_weight(w)
            if w == PASSES:
                for n, rows in enumerate(out_vectors):
                    nc.sync.dma_start(out=out_vec_rows[n * O_GROUPS : (n + 1) * O_GROUPS, :], in_=rows)
        direct_cols = slice(DIRECT_GROUP * BANK, (DIRECT_GROUP + 1) * BANK)
        for n, vector in enumerate((u1[0, direct_cols], u1_R[0, direct_cols], bias[direct_cols])):
            nc.sync.dma_start(out=direct_vectors[:, n, :], in_=vector.partition_broadcast(P))

        v_codes = [keep.tile([P, S_TILES, K_PASS], U32, name="v_codes%d" % b, align_bytes=64) for b in range(2)]
        v_scales = [keep.tile([P, S_TILES, K_PASS], U8, name="v_scales%d" % b, align_bytes=64) for b in range(2)]
        u_codes = [keep.tile([P, O_GROUPS, BANK], U32, name="u_codes%d" % b, align_bytes=64) for b in range(2)]
        u_scales = [keep.tile([P, O_GROUPS, BANK], U8, name="u_scales%d" % b, align_bytes=64) for b in range(2)]
        x_codes = {}
        x_scales = {}
        h_codes = {}
        h_scales = {}
        for pair in range(HALVES * PAIRS):
            x_codes[pair] = keep.tile([P, PASSES, BRANCHES * PAIR], U32, name="x_codes%d" % pair, align_bytes=64)
            x_scales[pair] = keep.tile([P, PASSES, BRANCHES * PAIR], U8, name="x_scales%d" % pair, align_bytes=64)
        for b in range(BRANCHES):
            for h in range(HALVES):
                h_codes[b, h] = keep.tile([P, BANK], U32, name="h_codes%d%d" % (b, h), align_bytes=64)
                h_scales[b, h] = keep.tile([P, BANK], U8, name="h_scales%d%d" % (b, h), align_bytes=64)

        signed = []
        scaled_x = []

        def sign_weight(w):
            words = raw_w[w][:].bitcast(F32)
            signs = stage.tile([P, UNITS * P, PACK], BF16, tag="signs", bufs=3, align_bytes=64)
            for i in range(UNITS // 2):
                bank = psum.tile([P, BANK], F32, tag="bank", name="bank")
                for u in range(2):
                    for n in range(2):
                        first = (2 * (2 * i + n) + u) * P
                        nc.tensor.transpose(
                            bank[:, (2 * u + n) * P : (2 * u + n + 1) * P], words[:, first : first + P], ident_f32[:]
                        )
                nc.scalar.activation(
                    out=signs[:, i * 2 * P : (i + 1) * 2 * P, :].rearrange("p q (u e) -> p q u e", u=2),
                    in_=bank[:].bitcast(BF16).rearrange("p (u q e) -> p q u e", u=2, e=2),
                    func=ACT.Sign,
                )
            signed.append((w, signs))

        def quantise_weights(keep):
            while len(signed) > keep:
                w, signs = signed.pop(0)
                if w < V_WEIGHTS:
                    b, t = w // S_TILES, w % S_TILES
                    codes, scales = v_codes[b][:, t, :], v_scales[b][:, t, :]
                else:
                    og, b = (w - V_WEIGHTS) // BRANCHES, w % BRANCHES
                    codes, scales = u_codes[b][:, og, :], u_scales[b][:, og, :]
                nc.vector.quantize_mx(
                    out=codes.bitcast(FP8X4), scales=scales, in_=signs[:].rearrange("p q t -> p (q t)")
                )

        def scale_x(pair, g):
            words = x_words[pair, g]
            bank = psum.tile([P, BANK], F32, tag="bank", name="bank")
            for u in range(2):
                for i in range(2):
                    nc.tensor.transpose(
                        bank[:, (2 * u + i) * P : (2 * u + i + 1) * P], words[:, i, u * P : (u + 1) * P], ident_f32[:]
                    )
            scaled = stage.tile([P, BRANCHES, PAIR, PACK], BF16, tag="scaled", bufs=4, align_bytes=64)
            for b in range(BRANCHES):
                first = (b * PASSES + g) * PACK
                factors = k_vectors[:, first : first + PACK].rearrange("p (u e) -> p u e", u=2)
                nc.vector.tensor_tensor(
                    out=scaled[:, b, :, :].rearrange("p r (u e) -> p r u e", u=2),
                    in0=bank[:].bitcast(BF16).rearrange("p (u r e) -> p r u e", u=2, e=2),
                    in1=factors.unsqueeze(1).to_broadcast([P, PAIR, 2, 2]),
                    op=ALU.mult,
                )
            scaled_x.append((pair, g, scaled))

        def quantise_x(keep):
            while len(scaled_x) > keep:
                pair, g, scaled = scaled_x.pop(0)
                nc.vector.quantize_mx(
                    out=x_codes[pair][:, g, :].bitcast(FP8X4),
                    scales=x_scales[pair][:, g, :],
                    in_=scaled[:].rearrange("p b r t -> p (b r t)"),
                )

        grouped_h = {}

        def first_stage(h, b, i):
            if i == 0:
                grouped_h[h, b] = stage.tile([P, BANK, PACK], BF16, tag="grouped", name="grouped", align_bytes=64)
            rows = slice(i * P, (i + 1) * P)
            pair = (h * BANK + i * P) // PAIR
            first = b * PAIR + (i * P) % PAIR
            x_cols = slice(first, first + P)
            acc = psum.tile([P, S_TILES, P], F32, tag="bank", name="bank")
            for t in range(S_TILES):
                for g in range(PASSES):
                    nc.tensor.matmul_mx(
                        out=acc[:, t, :],
                        lhsT=v_codes[b][:, t, g * P : (g + 1) * P].bitcast(FP8X4),
                        lhsT_scale=v_scales[b][:, t, g * P : (g + 1) * P],
                        rhs=x_codes[pair][:, g, x_cols].bitcast(FP8X4),
                        rhs_scale=x_scales[pair][:, g, x_cols],
                        start=(g == 0),
                        stop=(g == PASSES - 1),
                    )
            nc.vector.tensor_tensor(
                out=grouped_h[h, b][:, rows, :],
                in0=acc[:].rearrange("p t r -> p r t"),
                in1=v1u2[:, b, :].unsqueeze(1).to_broadcast([P, P, PACK]),
                op=ALU.mult,
            )

        def quantise_h(h, b):
            nc.vector.quantize_mx(
                out=h_codes[b, h][:].bitcast(FP8X4),
                scales=h_scales[b, h][:],
                in_=grouped_h[h, b][:].rearrange("p r t -> p (r t)"),
            )

        totals = {}

        def product(h, og, b, ol):
            acc = psum.tile([P, BANK], F32, tag="bank", name="bank")
            nc.tensor.matmul_mx(
                out=acc[:],
                lhsT=u_codes[b][:, og, ol * P : (ol + 1) * P].bitcast(FP8X4),
                lhsT_scale=u_scales[b][:, og, ol * P : (ol + 1) * P],
                rhs=h_codes[b, h][:].bitcast(FP8X4),
                rhs_scale=h_scales[b, h][:],
                start=True,
                stop=True,
            )
            return acc

        def main_branch(h, og, ol):
            if ol == 0:
                totals[h, og] = stage.tile([P, O_TILES, BANK], F32, tag="total", name="total", bufs=3)
            nc.scalar.activation(
                out=totals[h, og][:, ol, :],
                in_=product(h, og, 0, ol)[:],
                func=ACT.Identity,
                scale=o_vectors[:, og, ol : ol + 1],
                bias=o_vectors[:, 2 * O_GROUPS + og, ol : ol + 1],
            )

        direct_results = []

        def direct(h, og, j):
            rows = slice(j * P, (j + 1) * P)
            terms = raws_w.tile([P, IN], BF16, tag="raw_w", name="terms")[:].bitcast(F32)
            terms = terms.rearrange("p (b o) -> p b o", b=BRANCHES)
            for b in range(BRANCHES):
                acc = psum.tile([P, BANK], F32, tag="bank", name="bank")
                nc.tensor.matmul_mx(
                    out=acc[:],
                    lhsT=h_codes[b, h][:, rows].bitcast(FP8X4),
                    lhsT_scale=h_scales[b, h][:, rows],
                    rhs=u_codes[b][:, og, :].bitcast(FP8X4),
                    rhs_scale=u_scales[b][:, og, :],
                    start=True,
                    stop=True,
                )
                nc.vector.tensor_tensor(
                    out=terms[:, b, :].rearrange("p (q n) -> p q n", n=O_TILES),
                    in0=acc[:].rearrange("p (n q) -> p q n", n=O_TILES),
                    in1=direct_vectors[:, b, :].rearrange("p (q n) -> p q n", n=O_TILES),
                    op=ALU.mult,
                )
            nc.gpsimd.tensor_tensor(out=terms[:, 0, :], in0=terms[:, 0, :], in1=terms[:, 1, :], op=ALU.add)
            nc.gpsimd.tensor_tensor(out=terms[:, 0, :], in0=terms[:, 0, :], in1=direct_vectors[:, BRANCHES, :], op=ALU.add)
            direct_results.append((h, og, j, terms))

        def store_direct(h, og, j, terms):
            r0 = h * BANK + j * P
            nc.sync.dma_start(out=out_rows[r0 : r0 + P, og * BANK : (og + 1) * BANK], in_=terms[:, 0, :])

        def add_residual_branch(h, og, ol):
            nc.vector.scalar_tensor_tensor(
                out=totals[h, og][:, ol, :],
                in0=product(h, og, 1, ol)[:],
                scalar=o_vectors[:, O_GROUPS + og, ol : ol + 1],
                in1=totals[h, og][:, ol, :],
                op0=ALU.mult,
                op1=ALU.add,
            )

        def store(h, og, j):
            bank = psum.tile([P, BANK], F32, tag="bank", name="bank")
            for ol in range(O_TILES):
                nc.tensor.transpose(
                    bank[:, ol * P : (ol + 1) * P], totals[h, og][:, ol, j * P : (j + 1) * P], ident_f32[:]
                )
            result = stage.tile([P, BANK], F32, tag="result", name="result", bufs=8)
            by_tile = bank[:].rearrange("p (n q) -> p q n", n=O_TILES)
            in_order = result[:].rearrange("p (q n) -> p q n", n=O_TILES)
            if h == HALVES - 1 and og >= O_GROUPS - 2 and j % 2 == 1:
                nc.vector.tensor_copy(out=in_order, in_=by_tile)
            else:
                nc.scalar.copy(out=in_order, in_=by_tile)
            r0 = h * BANK + j * P
            nc.sync.dma_start(out=out_rows[r0 : r0 + P, og * BANK : (og + 1) * BANK], in_=result[:])

        x_passes = [(pair, g) for pair in range(HALVES * PAIRS) for g in range(PASSES)]
        h_units = [
            (h, b, 2 * pair + i)
            for h in range(HALVES)
            for pair in range(PAIRS)
            for b in range(BRANCHES)
            for i in range(2)
        ]

        full_h = []

        def next_first_stage():
            h, b, i = h_units.pop(0)
            first_stage(h, b, i)
            quantise_full_h()
            if i == X_TILES - 1:
                full_h.append((h, b))

        def quantise_full_h():
            while full_h:
                quantise_h(*full_h.pop(0))

        word_bank = psum.tile([P, BANK], F32, tag="bank", name="bank")
        nc.tensor.transpose(word_bank[:, 0:P], word_rows[:].bitcast(F32), ident_f32[:])
        k_vectors = consts.tile([P, WORD_COLS], BF16)
        nc.vector.tensor_copy(out=k_vectors[:], in_=word_bank[:].bitcast(BF16)[:, 0:WORD_COLS])
        V2_COLS = BRANCHES * PASSES * PACK
        v1_and_u2 = k_vectors[:, V2_COLS:WORD_COLS].rearrange("p (b w t) -> p b w t", b=BRANCHES, w=2)
        v1u2 = consts.tile([P, BRANCHES, PACK], F32)
        nc.vector.tensor_tensor(out=v1u2[:], in0=v1_and_u2[:, :, 0, :], in1=v1_and_u2[:, :, 1, :], op=ALU.mult)
        for w in range(V_WEIGHTS):
            scale_x(*x_passes.pop(0))
            sign_weight(w)
            quantise_x(keep=1)
            quantise_weights(keep=1)
        out_vec_bank = psum.tile([P, 2, P], F32, tag="bank", name="bank")
        for u in range(2):
            nc.tensor.transpose(out_vec_bank[:, u, :], out_vec_rows[:].bitcast(F32)[:, u::2], ident_f32[:])
        o_vectors = consts.tile([P, 3 * O_GROUPS, O_TILES], F32)
        nc.vector.tensor_copy(
            out=o_vectors[:].rearrange("p r (u e) -> p u r e", u=2),
            in_=out_vec_bank[:].bitcast(BF16).rearrange("p u (r e) -> p u r e", e=2)[:, :, 0 : 3 * O_GROUPS, :],
        )
        next_u = V_WEIGHTS
        for n in range(BRANCHES * X_TILES):
            if n % 4 == 2:
                scale_x(*x_passes.pop(0))
                quantise_x(keep=1)
            if n % 2 == 0:
                sign_weight(next_u)
                next_u += 1
            if n == 0:
                quantise_x(keep=0)
                quantise_weights(keep=1)
            next_first_stage()
            quantise_weights(keep=1)
        quantise_full_h()
        steps = [(h, og, ol) for h in range(HALVES) for og in range(O_GROUPS) for ol in range(O_TILES)]
        mains = [(h, og, ol) for h, og, ol in steps if (h, og) != (HALVES - 1, DIRECT_GROUP)]
        main_count = len(mains)
        waiting = []
        for step, (h, og, ol) in enumerate(steps):
            while main_count - len(mains) < min(step + 2, main_count):
                main_branch(*mains.pop(0))
            if (h, og) == (HALVES - 1, DIRECT_GROUP):
                direct(h, og, ol)
            else:
                add_residual_branch(h, og, ol)
                if direct_results and step % 3 == 2:
                    store_direct(*direct_results.pop(0))
            quantise_full_h()
            if ol % 2 == 1:
                for tile in range(min(2, len(waiting))):
                    store(*waiting.pop(0))
            if h == 0:
                if step % 2 == 1 and next_u < WEIGHTS:
                    sign_weight(next_u)
                    next_u += 1
                if (step == 0 or step % 2 == 1) and x_passes:
                    scale_x(*x_passes.pop(0))
                    quantise_x(keep=1)
                if not x_passes:
                    quantise_x(keep=0)
                if step > 5 and step % 2 == 1:
                    for unit in range(min(2, len(h_units))):
                        next_first_stage()
                quantise_weights(keep=0 if ol == O_TILES - 1 else 1)
            if ol == O_TILES - 1 and (h, og) != (HALVES - 1, DIRECT_GROUP):
                waiting += [(h, og, j) for j in range(X_TILES)]
        for tile in waiting:
            store(*tile)
